import numpy as np
import ml_dtypes


def mxq(x, axis, fmt="e4m3"):
    dtype, down = {"e4m3": (ml_dtypes.float8_e4m3fn, 7), "e5m2": (ml_dtypes.float8_e5m2, 14)}[fmt]
    v = np.moveaxis(np.asarray(x, np.float32).astype(ml_dtypes.bfloat16).astype(np.float64), axis, -1)
    blocks = v.reshape(v.shape[:-1] + (-1, 32))
    amax = np.abs(blocks).max(-1, keepdims=True)
    byte = np.maximum(np.where(amax > 0, np.frexp(amax)[1] - 1 + 127, 0) - down, 1)
    scale = np.exp2(byte - 127.0)
    codes = (blocks / scale).astype(np.float32).astype(dtype).astype(np.float64)
    return np.moveaxis((codes * scale).reshape(v.shape), -1, axis)


WIDE = False


def mx_kscale(k):
    if not WIDE:
        return np.ones(k)
    levels = np.array([18, -18])
    if k % 512:
        return np.exp2(np.random.permutation(np.resize(levels, k // 32))).repeat(32)
    a = np.empty((k // 512, 16))
    for p in range(k // 512):
        a[p, :8] = np.random.permutation(np.resize(levels, 8))
        for g in range(8):
            far = levels[np.abs(levels - a[p, g]) >= 10]
            a[p, g + 8] = far[np.random.randint(len(far))]
    return np.exp2(a.ravel()).repeat(32)


BF16 = ml_dtypes.bfloat16


def bf(x):
    return np.asarray(x, np.float32).astype(BF16)


def f64(x):
    return np.asarray(x).astype(np.float64)


B, CL, CH, CK, CV, CO, H, W = 2, 1024, 2048, 256, 512, 1024, 32, 32
N = H * W
T = B * N
CF = CO + CH
EPS = 1e-5


def setup_inputs():
    s = mx_kscale(T).reshape(B, 1, H, W)
    u = mx_kscale(CO)
    v = mx_kscale(CO)
    vc = np.concatenate([v, np.ones(CH)])
    x0 = bf(np.random.standard_normal((B, CV, H, W)) * 0.4)
    hi = bf(np.random.standard_normal((B, CH, H, W)))
    ww0 = bf(np.random.standard_normal((CO, CV)) * 2.0 / np.sqrt(CV))
    bw = bf(np.random.standard_normal(CO) * 0.3)
    wf0 = bf(np.random.standard_normal((CO, CF)) / np.sqrt(CF))
    bfuse = bf(np.random.standard_normal(CO) * 0.3)
    gf = bf(np.random.uniform(0.5, 1.5, CO))
    bef = bf(np.random.standard_normal(CO) * 0.3)
    mf = bf(np.random.standard_normal(CO) * 0.3)
    vf = bf(np.random.uniform(0.5, 1.5, CO))
    g = bf(np.random.standard_normal((B, CO, H, W)) * np.exp2(np.random.randint(-6, 1, (B, 1, H, W))) / s * u[None, :, None, None])
    rstd = 1.0 / np.sqrt(f64(vf) + EPS)
    return {"context": bf(f64(x0) * s),
            "high_feats": hi,
            "ww": bf(f64(ww0) / v[:, None]),
            "bw": bw,
            "wf": bf(f64(wf0) * vc[None, :] / u[:, None]),
            "bfuse": bfuse,
            "gf": gf,
            "bef": bef,
            "mf": mf,
            "vf": vf,
            "rstd": np.asarray(rstd, np.float32),
            "grad_out": g}


def reference(context, high_feats, ww, bw, wf, bfuse, gf, bef, mf, vf, rstd, grad_out):
    g = f64(grad_out).reshape(B, CO, N).transpose(1, 0, 2).reshape(CO, T)
    x = f64(context).reshape(B, CV, N).transpose(1, 0, 2).reshape(CV, T)
    dz2 = g * (f64(gf) * f64(rstd))[:, None]
    wc = f64(wf)[:, :CO]
    dz1 = mxq(wc, 0, "e4m3").T @ mxq(dz2, 0, "e5m2")
    dx = mxq(f64(ww), 0, "e4m3").T @ mxq(dz1, 0, "e5m2")
    dww = mxq(dz1, 1, "e5m2") @ mxq(x, 1, "e4m3").T
    dcontext = dx.reshape(CV, B, N).transpose(1, 0, 2).reshape(B, CV, H, W)
    return dcontext, dww

@@ -1,0 +1,299 @@
+from contextlib import ExitStack
+
+import concourse.mybir as mybir
+from concourse.masks import make_identity
+
+F32 = mybir.dt.float32
+BF16 = mybir.dt.bfloat16
+U32 = mybir.dt.uint32
+U8 = mybir.dt.uint8
+E4X4 = mybir.dt.float8_e4m3fn_x4
+E5X4 = mybir.dt.float8_e5m2_x4
+MULT = mybir.AluOpType.mult
+
+FLOPS = 2 * 2048 * (1024 * 1024 + 2 * 1024 * 512)
+BYTES = 2 * (2048 * 1024 + 2048 * 512 + 1024 * 1024 + 1024 * 512) + 4 * (2048 * 512 + 1024 * 512)
+
+
+LOADS = """
+lg.01 lw.00 lg.00 lw.01 lw.10 lu.1 lw.11 lx.0 lg.20 lg.31 lg.10 lx.1 lu.0 lx.3 lg.11 lg.30 lx.2 lg.21
+"""
+PLAN = """
+sc.01 gi.01.V wi.00.S sc.00 gq.01 wi.01.S gi.00.V wq.00 gq.00 wq.01 ui.1.V wi.10.S wi.11.V b.00.VSSS
+il.00.S wq.11 wq.10 xt.0.VV uq.1 qc.00 tr.00.VV xq.0 qt.00 b.10.SSSS xt.1.SS sc.10 ui.0.S gi.10.S
+il.10.V sc.20 xq.1 tr.10.SS uq.0 xt.3.SV sc.11 qc.10 gi.20.S sc.21 gq.10 qt.10 gi.11.V xq.3
+gq.11 o.0.SSSS sc.31 gi.21.S sc.30 xt.2.VV b.01.VSSS il.01.S gq.21 gq.20 b.11.VVVV b.02.SVVS xq.2 il.11.V
+tr.01.SS qc.01 qc.11 gi.30.V tr.11.SS gi.31.S b.12.SVSS gq.30 gq.31 o.1.VVVS il.02.V qt.01 tr.02.SS qt.02
+qt.11 b.03.SSSS b.13.SVSS tr.03.SV tr.13.VS qt.03 qc.02 il.12.V il.03.S qc.12 tr.12.SV qc.03 wz.0.SSSS il.13.V
+qc.13 qt.13 o.2.VSSS qt.12 o.3.SSVS wz.1.VSSS
+"""
+
+
+def tile_afnb_pb_v_kernel(
+    tc, context, high_feats, ww, bw, wf, bfuse, gf, bef, mf, vf, rstd, grad_out, out_0, out_1
+):
+    nc = tc.nc
+    g_v = grad_out.rearrange("b (q p j) h w -> b q p j (h w)", q=2, j=4)
+    x_v = context.rearrange("b (r p) h w -> b p r (h w)", p=128)
+    wf_v = wf.rearrange("(q p j) c -> q p j c", q=2, j=4)
+    ww_v = ww.rearrange("(q p j) v -> q p j v", q=2, j=4)
+    out0_v = out_0.rearrange("b (r p) h w -> b r p (h w)", p=128)
+    out1_v = out_1.rearrange("(h m t) v -> h t m v", h=2, t=4)
+
+    with ExitStack() as ctx:
+        keep = ctx.enter_context(tc.tile_pool(name="keep", bufs=1))
+        work = ctx.enter_context(tc.tile_pool(name="work", bufs=3))
+        psum = ctx.enter_context(tc.psum_pool(name="psum", bufs=8))
+
+        def bank():
+            t = psum.tile([128, 512], F32, name="bank")
+            return t
+
+        def evac(eng, out, in_):
+            if eng == "S":
+                nc.scalar.copy(out=out, in_=in_)
+            else:
+                nc.vector.tensor_copy(out=out, in_=in_)
+
+        def coded(name, q):
+            codes = keep.tile([128, 512], U32, name=name + "c" + str(q), align_bytes=64)
+            scales = keep.tile([128, 512], U8, name=name + "s" + str(q), align_bytes=64)
+            return codes, scales
+
+        def quant(dst, fmt, src):
+            nc.vector.quantize_mx(
+                out=dst[0][:].bitcast(fmt), scales=dst[1][:], in_=src[:].rearrange("p n j -> p (n j)")
+            )
+
+        def inter():
+            t = work.tile([128, 512, 4], BF16, name="inter", align_bytes=64, bufs=6)
+            return t
+
+        def interleave(eng, dst, src):
+            evac(
+                eng,
+                dst[:].rearrange("p (c i) j -> p c j i", i=4),
+                src[:].rearrange("p j (c i) -> p c j i", i=4),
+            )
+
+        ident = keep.tile([128, 128], F32, name="ident")
+        make_identity(nc, ident[:])
+
+        gf_t = keep.tile([128, 2, 4], BF16, name="gf_t")
+        rs_t = keep.tile([128, 2, 4], F32, name="rs_t")
+        s_t = keep.tile([128, 8], F32, name="s_t")
+        nc.scalar.dma_start(out=gf_t[:], in_=gf.rearrange("(q p j) -> p q j", q=2, j=4))
+        nc.scalar.dma_start(out=rs_t[:], in_=rstd.rearrange("(q p j) -> p q j", q=2, j=4))
+        nc.vector.tensor_tensor(
+            out=s_t[:],
+            in0=gf_t[:].rearrange("p q j -> p (q j)"),
+            in1=rs_t[:].rearrange("p q j -> p (q j)"),
+            op=MULT,
+        )
+
+        wraw, graw, xraw, uraw = {}, {}, {}, {}
+
+        def load_w(h, q):
+            t = keep.tile([128, 4, 512], BF16, name="wraw" + str(h) + str(q))
+            nc.sync.dma_start(out=t[:], in_=wf_v[q, :, :, 512 * h : 512 * h + 512])
+            wraw[h, q] = t
+
+        def load_g(T, q):
+            t = keep.tile([128, 4, 512], BF16, name="graw" + str(T) + str(q))
+            n0 = 512 * (T % 2)
+            nc.sync.dma_start(out=t[:], in_=g_v[T // 2, q, :, :, n0 : n0 + 512])
+            graw[T, q] = t
+
+        def load_x(T):
+            t = keep.tile([128, 4, 512], BF16, name="xraw" + str(T))
+            n0 = 512 * (T % 2)
+            nc.sync.dma_start(out=t[:], in_=x_v[T // 2, :, :, n0 : n0 + 512])
+            xraw[T] = t
+
+        def load_u(q):
+            t = keep.tile([128, 4, 512], BF16, name="uraw" + str(q))
+            nc.sync.dma_start(out=t[:], in_=ww_v[q])
+            uraw[q] = t
+
+
+        wq, gq, xq, uq, ckq, tkq, E, Z, D = {}, {}, {}, {}, {}, {}, {}, {}, {}
+
+        def words(d):
+            return d[:].rearrange("p n j -> p (n j)").bitcast(F32).rearrange("p (a b u) -> p a b u", a=4, u=2)
+
+        def mm(bk, a, ac, b, start, stop, fa, fb):
+            nc.tensor.matmul_mx(
+                out=bk[:],
+                lhsT=a[0][:, ac].bitcast(fa),
+                lhsT_scale=a[1][:, ac],
+                rhs=b[0][:].bitcast(fb),
+                rhs_scale=b[1][:],
+                start=start,
+                stop=stop,
+            )
+
+        def cols(t):
+            return slice(128 * t, 128 * t + 128)
+
+        def wi(h, q, eng):
+            d = inter()
+            D["w", h, q] = d
+            evac(
+                eng,
+                d[:].rearrange("p (t m) j -> p t m j", t=4),
+                wraw[h, q][:].rearrange("p j (m t) -> p t m j", t=4),
+            )
+
+        def w_quant(h, q):
+            wq[h, q] = coded("w" + str(h), q)
+            quant(wq[h, q], E4X4, D["w", h, q])
+
+        def ui(q, eng):
+            d = inter()
+            D["u", q] = d
+            interleave(eng, d, uraw[q])
+
+        def u_quant(q):
+            uq[q] = coded("u", q)
+            quant(uq[q], E4X4, D["u", q])
+
+        def sc(T, q):
+            z = work.tile([128, 4, 512], BF16, name="dz2", bufs=3)
+            Z[T, q] = z
+            for j in range(4):
+                nc.vector.tensor_scalar(
+                    out=z[:, j, :],
+                    in0=graw[T, q][:, j, :],
+                    scalar1=s_t[:, 4 * q + j : 4 * q + j + 1],
+                    scalar2=None,
+                    op0=MULT,
+                )
+
+        def gi(T, q, eng):
+            d = inter()
+            D["g", T, q] = d
+            interleave(eng, d, Z[T, q])
+
+        def g_quant(T, q):
+            gq[T, q] = coded("g" + str(T), q)
+            quant(gq[T, q], E5X4, D["g", T, q])
+
+        def xt(T, engs):
+            d = inter()
+            D["x", T] = d
+            for h in range(2):
+                bk = bank()
+                for r in range(2):
+                    for u in range(2):
+                        nc.tensor.transpose(
+                            bk[:, 256 * r + 128 * u : 256 * r + 128 * u + 128],
+                            xraw[T][:, 2 * h + r, :].bitcast(F32)[:, u:256:2],
+                            ident[:],
+                        )
+                evac(
+                    engs[h],
+                    words(d)[:, 2 * h : 2 * h + 2],
+                    bk[:].rearrange("p (r u v) -> p r v u", r=2, u=2),
+                )
+
+        def x_quant(T):
+            xq[T] = coded("x", T)
+            quant(xq[T], E4X4, D["x", T])
+
+        def b(h, T, engs):
+            e = work.tile([128, 4, 512], BF16, name="E", bufs=3)
+            E[h, T] = e
+            for t in range(4):
+                bk = bank()
+                for q in range(2):
+                    mm(bk, wq[h, q], cols(t), gq[T, q], q == 0, q == 1, E4X4, E5X4)
+                evac(
+                    engs[t],
+                    e[:, t, :].rearrange("p (u q e) -> p u q e", u=2, e=2),
+                    bk[:].rearrange("p (q u e) -> p u q e", u=2, e=2),
+                )
+
+        def tr(h, T, engs):
+            e = E[h, T]
+            d = inter()
+            D["t", h, T] = d
+            for hh in range(2):
+                bk = bank()
+                for r in range(2):
+                    for u in range(2):
+                        nc.tensor.transpose(
+                            bk[:, 256 * r + 128 * u : 256 * r + 128 * u + 128],
+                            e[:, 2 * hh + r, :].bitcast(F32)[:, 128 * u : 128 * u + 128],
+                            ident[:],
+                        )
+                evac(
+                    engs[hh],
+                    words(d)[:, 2 * hh : 2 * hh + 2],
+                    bk[:].rearrange("p (r u v) -> p r v u", r=2, u=2),
+                )
+
+        def il(h, T, eng):
+            d = inter()
+            D["c", h, T] = d
+            interleave(eng, d, E[h, T])
+
+        def qc(h, T):
+            ckq[h, T] = coded("ck" + str(h), T)
+            quant(ckq[h, T], E5X4, D["c", h, T])
+
+        def qt(h, T):
+            tkq[h, T] = coded("tk" + str(h), T)
+            quant(tkq[h, T], E5X4, D["t", h, T])
+
+        def o(T, engs):
+            for r in range(4):
+                bk = bank()
+                for h in range(2):
+                    mm(bk, uq[h], cols(r), ckq[h, T], h == 0, h == 1, E4X4, E5X4)
+                res = work.tile([128, 512], F32, name="res", bufs=6)
+                evac(
+                    engs[r],
+                    res[:].rearrange("p (q u e) -> p q u e", u=2, e=2),
+                    bk[:].rearrange("p (u q e) -> p q u e", u=2, e=2),
+                )
+                n0 = 512 * (T % 2)
+                nc.sync.dma_start(out=out0_v[T // 2, r, :, n0 : n0 + 512], in_=res[:])
+
+        wbank = {}
+
+        def wa(h, T):
+            for t in range(4):
+                if T == 0:
+                    wbank[h, t] = bank()
+                mm(wbank[h, t], tkq[h, T], cols(t), xq[T], T == 0, False, E5X4, E4X4)
+
+        def wz(h, engs, T0=0):
+            for t in range(4):
+                if T0 == 0:
+                    wbank[h, t] = bank()
+                for T in range(T0, 4):
+                    mm(wbank[h, t], tkq[h, T], cols(t), xq[T], T == 0, T == 3, E5X4, E4X4)
+                res = work.tile([128, 512], F32, name="res", bufs=6)
+                evac(engs[t], res[:], wbank[h, t][:])
+                nc.sync.dma_start(out=out1_v[h, t], in_=res[:])
+
+        ops = {
+            "lw": load_w, "lg": load_g, "lx": load_x, "lu": load_u,
+            "wi": wi, "wq": w_quant, "ui": ui, "uq": u_quant, "sc": sc, "gi": gi, "gq": g_quant,
+            "xt": xt, "xq": x_quant, "b": b, "tr": tr, "il": il, "qc": qc, "qt": qt, "o": o, "wa": wa, "wz": wz,
+        }
+
+        def runs(token):
+            parts = token.split(".")
+            args = [int(c) for c in parts[1]]
+            if len(parts) > 2:
+                args.append(parts[2])
+            if len(parts) > 3:
+                args.append(int(parts[3]))
+            ops[parts[0]](*args)
+
+        for token in LOADS.split():
+            runs(token)
+        with tc.manual_schedule():
+            for token in PLAN.split():
+                runs(token)

@@ -15,17 +15,29 @@ FLOPS = 2 * 2048 * (1024 * 1024 + 2 * 1024 * 512)
 BYTES = 2 * (2048 * 1024 + 2048 * 512 + 1024 * 1024 + 1024 * 512) + 4 * (2048 * 512 + 1024 * 512)
 
 
+NINTER = 9
+NRAW = 8
+NE = 4
 LOADS = """
-lg.01 lw.00 lg.00 lw.01 lw.10 lu.1 lw.11 lx.0 lg.20 lg.31 lg.10 lx.1 lu.0 lx.3 lg.11 lg.30 lx.2 lg.21
+lg.00 lw.00 lg.01 lw.10 lw.01 lg.10 lg.11 lw.11 lG.10 lG.11 lx.1 lx.0 lu.1 lu.0
 """
 PLAN = """
-sc.01 gi.01.V wi.00.S sc.00 gq.01 wi.01.S gi.00.V wq.00 gq.00 wq.01 ui.1.V wi.10.S wi.11.V b.00.VSSS
-il.00.S wq.11 wq.10 xt.0.VV uq.1 qc.00 tr.00.VV xq.0 qt.00 b.10.SSSS xt.1.SS sc.10 ui.0.S gi.10.S
-il.10.V sc.20 xq.1 tr.10.SS uq.0 xt.3.SV sc.11 qc.10 gi.20.S sc.21 gq.10 qt.10 gi.11.V xq.3
-gq.11 o.0.SSSS sc.31 gi.21.S sc.30 xt.2.VV b.01.VSSS il.01.S gq.21 gq.20 b.11.VVVV b.02.SVVS xq.2 il.11.V
-tr.01.SS qc.01 qc.11 gi.30.V tr.11.SS gi.31.S b.12.SVSS gq.30 gq.31 o.1.VVVS il.02.V qt.01 tr.02.SS qt.02
-qt.11 b.03.SSSS b.13.SVSS tr.03.SV tr.13.VS qt.03 qc.02 il.12.V il.03.S qc.12 tr.12.SV qc.03 wz.0.SSSS il.13.V
-qc.13 qt.13 o.2.VSSS qt.12 o.3.SSVS wz.1.VSSS
+st. sc.00 gi.000.V wi.001.S gi.001.V sc.01 gi.011.S gq.00 wq.001 gi.010.V wi.000.S wi.101.V gq.01 wi.100.S
+wq.000 wq.100 wq.101 wi.010.S wq.010 wi.011.S sc.10 b.000.S wq.011 gi.100.V b.001.S sc.11 gi.101.V gi.111.V
+b.003.S tr.000.S gi.110.S b.002.S gq.10 wi.111.S gq.11 wi.110.S il.001.V b.012.S wq.111 il.000.V b.010.S wq.110
+sc.30 sc.20 b.102.S b.013.S gi.301.V b.103.S sc.21 gi.300.V b.101.S gi.210.V sc.31 b.110.S b.111.S b.100.S
+gi.211.V b.112.S gi.310.V b.011.S b.113.S gq.21 qc.00 tr.001.S gi.200.V qt.000 xt.21.S qt.001 gi.311.V gi.201.S
+tr.110.S gq.30 gq.31 xt.20.S xq.2 tr.111.S ui.00.V gq.20 tr.101.S qt.111 il.011.V tr.100.S xt.31.S xt.10.S
+xt.00.S xt.11.S il.101.V il.010.V il.100.V tr.010.S tr.011.S xt.01.S xt.30.S qt.110 b.032.S ui.10.V b.033.S b.132.S
+b.131.S ui.01.V b.030.S ui.11.V uq.0 qc.10 uq.1 b.023.S b.130.S il.110.V b.021.S b.020.S b.022.S qt.100
+b.133.S b.031.S il.111.V b.123.V b.120.S b.122.V o.00.V qt.101 qc.01 o.01.S b.121.S o.02.S qc.11 o.03.S
+tr.030.S tr.020.S xq.3 tr.031.S tr.130.S xq.1 tr.120.V xq.0 tr.121.S qt.130 qt.030 tr.131.S tr.021.S o.13.S
+qt.120 o.11.S qt.121 o.10.S qt.020 o.12.S il.130.V wa.120 wa.100 wa.101 wa.110 wa.000 qt.010 qt.011
+wa.111 wa.112 wa.113 wa.102 il.030.S il.131.V wa.130 il.031.V wa.001 wa.103 qt.131 wa.121 wa.002 wv.11.S
+qc.13 wa.003 qc.03 il.021.V wa.122 wa.123 il.020.V wv.10.S wa.131 il.120.V wv.00.S il.121.V wv.12.S wa.132
+wa.010 wa.133 wv.13.S o.33.S o.30.S wa.011 qc.02 wa.012 qc.12 wa.013 wv.01.S o.32.S o.31.S qt.021
+wa.020 wa.030 o.20.S o.23.V o.21.S wa.021 qt.031 o.22.S wa.022 wa.023 wa.031 wa.032 wa.033 wv.02.V
+wv.03.S
 """
 
 
@@ -55,68 +67,80 @@ def tile_afnb_pb_v_kernel(
             else:
                 nc.vector.tensor_copy(out=out, in_=in_)
 
-        def coded(name, q):
-            codes = keep.tile([128, 512], U32, name=name + "c" + str(q), align_bytes=64)
-            scales = keep.tile([128, 512], U8, name=name + "s" + str(q), align_bytes=64)
+        def coded(name, bufs):
+            codes = work.tile([128, 512], U32, name=name + "_codes", align_bytes=64, bufs=bufs)
+            scales = work.tile([128, 512], U8, name=name + "_scales", align_bytes=64, bufs=bufs)
             return codes, scales
 
-        def quant(dst, fmt, src):
+        def quant(dst, fmt, src, n0=0, n1=512):
             nc.vector.quantize_mx(
-                out=dst[0][:].bitcast(fmt), scales=dst[1][:], in_=src[:].rearrange("p n j -> p (n j)")
+                out=dst[0][:, n0:n1].bitcast(fmt),
+                scales=dst[1][:, n0:n1],
+                in_=src[:, n0:n1, :].rearrange("p n j -> p (n j)"),
             )
 
         def inter():
-            t = work.tile([128, 512, 4], BF16, name="inter", align_bytes=64, bufs=6)
+            t = work.tile([128, 512, 4], BF16, name="inter", align_bytes=64, bufs=NINTER)
             return t
 
-        def interleave(eng, dst, src):
+        D = {}
+
+        def keyed(*key):
+            if key not in D:
+                D[key] = inter()
+            return D[key]
+
+        def interleave(eng, dst, src, f):
+            n = slice(256 * f, 256 * f + 256)
             evac(
                 eng,
-                dst[:].rearrange("p (c i) j -> p c j i", i=4),
-                src[:].rearrange("p j (c i) -> p c j i", i=4),
+                dst[:, n, :].rearrange("p (c i) j -> p c j i", i=4),
+                src[:, :, n].rearrange("p j (c i) -> p c j i", i=4),
             )
 
         ident = keep.tile([128, 128], F32, name="ident")
         make_identity(nc, ident[:])
+        ident_bf = keep.tile([128, 128], BF16, name="ident_bf")
+        make_identity(nc, ident_bf[:])
 
         gf_t = keep.tile([128, 2, 4], BF16, name="gf_t")
         rs_t = keep.tile([128, 2, 4], F32, name="rs_t")
         s_t = keep.tile([128, 8], F32, name="s_t")
-        nc.scalar.dma_start(out=gf_t[:], in_=gf.rearrange("(q p j) -> p q j", q=2, j=4))
-        nc.scalar.dma_start(out=rs_t[:], in_=rstd.rearrange("(q p j) -> p q j", q=2, j=4))
-        nc.vector.tensor_tensor(
-            out=s_t[:],
-            in0=gf_t[:].rearrange("p q j -> p (q j)"),
-            in1=rs_t[:].rearrange("p q j -> p (q j)"),
-            op=MULT,
-        )
+        nc.sync.dma_start(out=gf_t[:], in_=gf.rearrange("(q p j) -> p q j", q=2, j=4))
+        nc.sync.dma_start(out=rs_t[:], in_=rstd.rearrange("(q p j) -> p q j", q=2, j=4))
 
         wraw, graw, xraw, uraw = {}, {}, {}, {}
 
         def load_w(h, q):
-            t = keep.tile([128, 4, 512], BF16, name="wraw" + str(h) + str(q))
+            t = work.tile([128, 4, 512], BF16, name="raw", bufs=NRAW)
             nc.sync.dma_start(out=t[:], in_=wf_v[q, :, :, 512 * h : 512 * h + 512])
             wraw[h, q] = t
 
         def load_g(T, q):
-            t = keep.tile([128, 4, 512], BF16, name="graw" + str(T) + str(q))
+            t = work.tile([128, 4, 512], BF16, name="raw", bufs=NRAW)
             n0 = 512 * (T % 2)
             nc.sync.dma_start(out=t[:], in_=g_v[T // 2, q, :, :, n0 : n0 + 512])
-            graw[T, q] = t
+            graw[T, q] = t[:]
 
-        def load_x(T):
-            t = keep.tile([128, 4, 512], BF16, name="xraw" + str(T))
-            n0 = 512 * (T % 2)
-            nc.sync.dma_start(out=t[:], in_=x_v[T // 2, :, :, n0 : n0 + 512])
-            xraw[T] = t
+        def load_gg(b, q):
+            t = work.tile([128, 4, 1024], BF16, name="rawL", bufs=4)
+            nc.sync.dma_start(out=t[:], in_=g_v[b, q])
+            for i in range(2):
+                graw[2 * b + i, q] = t[:, :, 512 * i : 512 * i + 512]
+
+        def load_x(b):
+            t = work.tile([128, 4, 1024], BF16, name="rawL", bufs=4)
+            nc.sync.dma_start(out=t[:], in_=x_v[b])
+            for i in range(2):
+                xraw[2 * b + i] = t[:, :, 512 * i : 512 * i + 512]
 
         def load_u(q):
-            t = keep.tile([128, 4, 512], BF16, name="uraw" + str(q))
+            t = work.tile([128, 4, 512], BF16, name="rawu", bufs=2)
             nc.sync.dma_start(out=t[:], in_=ww_v[q])
             uraw[q] = t
 
 
-        wq, gq, xq, uq, ckq, tkq, E, Z, D = {}, {}, {}, {}, {}, {}, {}, {}, {}
+        wq, gq, xq, uq, ckq, tkq, E, Z, XD, TD = {}, {}, {}, {}, {}, {}, {}, {}, {}, {}
 
         def words(d):
             return d[:].rearrange("p n j -> p (n j)").bitcast(F32).rearrange("p (a b u) -> p a b u", a=4, u=2)
@@ -135,27 +159,35 @@ def tile_afnb_pb_v_kernel(
         def cols(t):
             return slice(128 * t, 128 * t + 128)
 
-        def wi(h, q, eng):
-            d = inter()
-            D["w", h, q] = d
+        def wi(h, q, f, eng):
+            bk = psum.tile([128, 2, 128, 4], BF16, name="bank")
+            src = wraw[h, q][:].rearrange("p j (m t) -> p t m j", t=4)
+            for i in range(2):
+                nc.tensor.matmul(
+                    out=bk[:, i].rearrange("p m j -> p (m j)"),
+                    lhsT=ident_bf[:],
+                    rhs=src[:, 2 * f + i],
+                    start=True,
+                    stop=True,
+                )
+            d = keyed("w", h, q)
             evac(
                 eng,
-                d[:].rearrange("p (t m) j -> p t m j", t=4),
-                wraw[h, q][:].rearrange("p j (m t) -> p t m j", t=4),
+                d[:, 256 * f : 256 * f + 256].rearrange("p n j -> p (n j)"),
+                bk[:].rearrange("p i m j -> p (i m j)"),
             )
 
-        def w_quant(h, q):
-            wq[h, q] = coded("w" + str(h), q)
-            quant(wq[h, q], E4X4, D["w", h, q])
+        def w_quant(h, q, f):
+            if (h, q) not in wq:
+                wq[h, q] = coded("w", 4)
+            quant(wq[h, q], E4X4, D["w", h, q], 256 * f, 256 * f + 256)
 
-        def ui(q, eng):
-            d = inter()
-            D["u", q] = d
-            interleave(eng, d, uraw[q])
+        def ui(q, f, eng):
+            interleave(eng, keyed("u", q, 0), uraw[q], f)
 
         def u_quant(q):
-            uq[q] = coded("u", q)
-            quant(uq[q], E4X4, D["u", q])
+            uq[q] = coded("u", 2)
+            quant(uq[q], E4X4, D["u", q, 0])
 
         def sc(T, q):
             z = work.tile([128, 4, 512], BF16, name="dz2", bufs=3)
@@ -169,118 +201,106 @@ def tile_afnb_pb_v_kernel(
                     op0=MULT,
                 )
 
-        def gi(T, q, eng):
-            d = inter()
-            D["g", T, q] = d
-            interleave(eng, d, Z[T, q])
+        def gi(T, q, f, eng):
+            interleave(eng, keyed("g", T, q), Z[T, q], f)
 
         def g_quant(T, q):
-            gq[T, q] = coded("g" + str(T), q)
+            gq[T, q] = coded("g", 6)
             quant(gq[T, q], E5X4, D["g", T, q])
 
-        def xt(T, engs):
-            d = inter()
-            D["x", T] = d
-            for h in range(2):
-                bk = bank()
-                for r in range(2):
-                    for u in range(2):
-                        nc.tensor.transpose(
-                            bk[:, 256 * r + 128 * u : 256 * r + 128 * u + 128],
-                            xraw[T][:, 2 * h + r, :].bitcast(F32)[:, u:256:2],
-                            ident[:],
-                        )
-                evac(
-                    engs[h],
-                    words(d)[:, 2 * h : 2 * h + 2],
-                    bk[:].rearrange("p (r u v) -> p r v u", r=2, u=2),
-                )
+        def xt(T, h, eng):
+            if T not in XD:
+                XD[T] = inter()
+            d = XD[T]
+            bk = bank()
+            for r in range(2):
+                for u in range(2):
+                    nc.tensor.transpose(
+                        bk[:, 256 * r + 128 * u : 256 * r + 128 * u + 128],
+                        xraw[T][:, 2 * h + r, :].bitcast(F32)[:, u:256:2],
+                        ident[:],
+                    )
+            evac(eng, words(d)[:, 2 * h : 2 * h + 2], bk[:].rearrange("p (r u v) -> p r v u", r=2, u=2))
 
         def x_quant(T):
-            xq[T] = coded("x", T)
-            quant(xq[T], E4X4, D["x", T])
+            xq[T] = coded("x", 4)
+            quant(xq[T], E4X4, XD[T])
 
-        def b(h, T, engs):
-            e = work.tile([128, 4, 512], BF16, name="E", bufs=3)
-            E[h, T] = e
-            for t in range(4):
-                bk = bank()
-                for q in range(2):
-                    mm(bk, wq[h, q], cols(t), gq[T, q], q == 0, q == 1, E4X4, E5X4)
-                evac(
-                    engs[t],
-                    e[:, t, :].rearrange("p (u q e) -> p u q e", u=2, e=2),
-                    bk[:].rearrange("p (q u e) -> p u q e", u=2, e=2),
-                )
+        def b(h, T, t, eng):
+            if (h, T) not in E:
+                E[h, T] = work.tile([128, 4, 512], BF16, name="E", bufs=NE)
+            bk = bank()
+            for q in range(2):
+                mm(bk, wq[h, q], cols(t), gq[T, q], q == 0, q == 1, E4X4, E5X4)
+            evac(
+                eng,
+                E[h, T][:, t, :].rearrange("p (u q e) -> p u q e", u=2, e=2),
+                bk[:].rearrange("p (q u e) -> p u q e", u=2, e=2),
+            )
 
-        def tr(h, T, engs):
+        def tr(h, T, hh, eng):
             e = E[h, T]
-            d = inter()
-            D["t", h, T] = d
-            for hh in range(2):
-                bk = bank()
-                for r in range(2):
-                    for u in range(2):
-                        nc.tensor.transpose(
-                            bk[:, 256 * r + 128 * u : 256 * r + 128 * u + 128],
-                            e[:, 2 * hh + r, :].bitcast(F32)[:, 128 * u : 128 * u + 128],
-                            ident[:],
-                        )
-                evac(
-                    engs[hh],
-                    words(d)[:, 2 * hh : 2 * hh + 2],
-                    bk[:].rearrange("p (r u v) -> p r v u", r=2, u=2),
-                )
+            if (h, T) not in TD:
+                TD[h, T] = inter()
+            bk = bank()
+            for r in range(2):
+                for u in range(2):
+                    nc.tensor.transpose(
+                        bk[:, 256 * r + 128 * u : 256 * r + 128 * u + 128],
+                        e[:, 2 * hh + r, :].bitcast(F32)[:, 128 * u : 128 * u + 128],
+                        ident[:],
+                    )
+            evac(eng, words(TD[h, T])[:, 2 * hh : 2 * hh + 2], bk[:].rearrange("p (r u v) -> p r v u", r=2, u=2))
 
-        def il(h, T, eng):
-            d = inter()
-            D["c", h, T] = d
-            interleave(eng, d, E[h, T])
+        def il(h, T, f, eng):
+            interleave(eng, keyed("c", h, T), E[h, T], f)
 
         def qc(h, T):
-            ckq[h, T] = coded("ck" + str(h), T)
+            ckq[h, T] = coded("ck", 5)
             quant(ckq[h, T], E5X4, D["c", h, T])
 
-        def qt(h, T):
-            tkq[h, T] = coded("tk" + str(h), T)
-            quant(tkq[h, T], E5X4, D["t", h, T])
+        def qt(h, T, f):
+            if (h, T) not in tkq:
+                tkq[h, T] = coded("tk", 8)
+            quant(tkq[h, T], E5X4, TD[h, T], 256 * f, 256 * f + 256)
 
-        def o(T, engs):
-            for r in range(4):
-                bk = bank()
-                for h in range(2):
-                    mm(bk, uq[h], cols(r), ckq[h, T], h == 0, h == 1, E4X4, E5X4)
-                res = work.tile([128, 512], F32, name="res", bufs=6)
-                evac(
-                    engs[r],
-                    res[:].rearrange("p (q u e) -> p q u e", u=2, e=2),
-                    bk[:].rearrange("p (u q e) -> p q u e", u=2, e=2),
-                )
-                n0 = 512 * (T % 2)
-                nc.sync.dma_start(out=out0_v[T // 2, r, :, n0 : n0 + 512], in_=res[:])
+        def o(T, r, eng):
+            bk = bank()
+            for h in range(2):
+                mm(bk, uq[h], cols(r), ckq[h, T], h == 0, h == 1, E4X4, E5X4)
+            res = work.tile([128, 512], F32, name="res", bufs=6)
+            evac(
+                eng,
+                res[:].rearrange("p (q u e) -> p q u e", u=2, e=2),
+                bk[:].rearrange("p (u q e) -> p q u e", u=2, e=2),
+            )
+            n0 = 512 * (T % 2)
+            nc.sync.dma_start(out=out0_v[T // 2, r, :, n0 : n0 + 512], in_=res[:])
 
         wbank = {}
 
-        def wa(h, T):
-            for t in range(4):
-                if T == 0:
-                    wbank[h, t] = bank()
-                mm(wbank[h, t], tkq[h, T], cols(t), xq[T], T == 0, False, E5X4, E4X4)
+        def wa(h, t, T):
+            if T == 0:
+                wbank[h, t] = bank()
+            mm(wbank[h, t], tkq[h, T], cols(t), xq[T], T == 0, T == 3, E5X4, E4X4)
 
-        def wz(h, engs, T0=0):
-            for t in range(4):
-                if T0 == 0:
-                    wbank[h, t] = bank()
-                for T in range(T0, 4):
-                    mm(wbank[h, t], tkq[h, T], cols(t), xq[T], T == 0, T == 3, E5X4, E4X4)
-                res = work.tile([128, 512], F32, name="res", bufs=6)
-                evac(engs[t], res[:], wbank[h, t][:])
-                nc.sync.dma_start(out=out1_v[h, t], in_=res[:])
+        def wv(h, t, eng):
+            res = work.tile([128, 512], F32, name="res", bufs=6)
+            evac(eng, res[:], wbank[h, t][:])
+            nc.sync.dma_start(out=out1_v[h, t], in_=res[:])
+
+        def st():
+            nc.vector.tensor_tensor(
+                out=s_t[:],
+                in0=gf_t[:].rearrange("p q j -> p (q j)"),
+                in1=rs_t[:].rearrange("p q j -> p (q j)"),
+                op=MULT,
+            )
 
         ops = {
-            "lw": load_w, "lg": load_g, "lx": load_x, "lu": load_u,
+            "lw": load_w, "lg": load_g, "lx": load_x, "lu": load_u, "lG": load_gg,
             "wi": wi, "wq": w_quant, "ui": ui, "uq": u_quant, "sc": sc, "gi": gi, "gq": g_quant,
-            "xt": xt, "xq": x_quant, "b": b, "tr": tr, "il": il, "qc": qc, "qt": qt, "o": o, "wa": wa, "wz": wz,
+            "xt": xt, "xq": x_quant, "b": b, "tr": tr, "il": il, "qc": qc, "qt": qt, "o": o, "wa": wa, "wv": wv, "st": st,
         }
 
         def runs(token):
@@ -288,8 +308,6 @@ def tile_afnb_pb_v_kernel(
             args = [int(c) for c in parts[1]]
             if len(parts) > 2:
                 args.append(parts[2])
-            if len(parts) > 3:
-                args.append(int(parts[3]))
             ops[parts[0]](*args)
 
         for token in LOADS.split():

@@ -15,29 +15,27 @@ FLOPS = 2 * 2048 * (1024 * 1024 + 2 * 1024 * 512)
 BYTES = 2 * (2048 * 1024 + 2048 * 512 + 1024 * 1024 + 1024 * 512) + 4 * (2048 * 512 + 1024 * 512)
 
 
-NINTER = 9
-NRAW = 8
-NE = 4
+NTURN = 5
+NRAW = 11
+NE = 5
 LOADS = """
-lg.00 lw.00 lg.01 lw.10 lw.01 lg.10 lg.11 lw.11 lG.10 lG.11 lx.1 lx.0 lu.1 lu.0
+
 """
 PLAN = """
-st. sc.00 gi.000.V wi.001.S gi.001.V sc.01 gi.011.S gq.00 wq.001 gi.010.V wi.000.S wi.101.V gq.01 wi.100.S
-wq.000 wq.100 wq.101 wi.010.S wq.010 wi.011.S sc.10 b.000.S wq.011 gi.100.V b.001.S sc.11 gi.101.V gi.111.V
-b.003.S tr.000.S gi.110.S b.002.S gq.10 wi.111.S gq.11 wi.110.S il.001.V b.012.S wq.111 il.000.V b.010.S wq.110
-sc.30 sc.20 b.102.S b.013.S gi.301.V b.103.S sc.21 gi.300.V b.101.S gi.210.V sc.31 b.110.S b.111.S b.100.S
-gi.211.V b.112.S gi.310.V b.011.S b.113.S gq.21 qc.00 tr.001.S gi.200.V qt.000 xt.21.S qt.001 gi.311.V gi.201.S
-tr.110.S gq.30 gq.31 xt.20.S xq.2 tr.111.S ui.00.V gq.20 tr.101.S qt.111 il.011.V tr.100.S xt.31.S xt.10.S
-xt.00.S xt.11.S il.101.V il.010.V il.100.V tr.010.S tr.011.S xt.01.S xt.30.S qt.110 b.032.S ui.10.V b.033.S b.132.S
-b.131.S ui.01.V b.030.S ui.11.V uq.0 qc.10 uq.1 b.023.S b.130.S il.110.V b.021.S b.020.S b.022.S qt.100
-b.133.S b.031.S il.111.V b.123.V b.120.S b.122.V o.00.V qt.101 qc.01 o.01.S b.121.S o.02.S qc.11 o.03.S
-tr.030.S tr.020.S xq.3 tr.031.S tr.130.S xq.1 tr.120.V xq.0 tr.121.S qt.130 qt.030 tr.131.S tr.021.S o.13.S
-qt.120 o.11.S qt.121 o.10.S qt.020 o.12.S il.130.V wa.120 wa.100 wa.101 wa.110 wa.000 qt.010 qt.011
-wa.111 wa.112 wa.113 wa.102 il.030.S il.131.V wa.130 il.031.V wa.001 wa.103 qt.131 wa.121 wa.002 wv.11.S
-qc.13 wa.003 qc.03 il.021.V wa.122 wa.123 il.020.V wv.10.S wa.131 il.120.V wv.00.S il.121.V wv.12.S wa.132
-wa.010 wa.133 wv.13.S o.33.S o.30.S wa.011 qc.02 wa.012 qc.12 wa.013 wv.01.S o.32.S o.31.S qt.021
-wa.020 wa.030 o.20.S o.23.V o.21.S wa.021 qt.031 o.22.S wa.022 wa.023 wa.031 wa.032 wa.033 wv.02.V
-wv.03.S
+lw.00 lg.00 lw.01 lg.01 lg.10 lw.10 lg.11 lw.11 lx.0 lG.10 lG.11 lx.1 lu.0 st.
+wi.00.V sc.00 wq.00 gi.00.V wi.01.S sc.01 gq.00 gi.01.V wq.01 gq.01 wi.10.S wi.11.S sc.10 b.000.S
+b.001.S b.002.S b.003.S gi.10.V sc.11 gq.10 gi.11.V wq.10 wq.11 xt.00.S xt.01.S tr.000.S tr.001.S lu.1
+lx.2 lx.3 sc.20 gq.11 b.100.S b.101.S b.102.S b.103.S b.010.S b.011.S b.012.S b.013.S gi.20.V sc.21
+gq.20 xq.0 gi.21.V qt.00 xt.10.S xt.11.S tr.010.S tr.011.S tr.100.S tr.101.S wa.000 wa.010 wa.020 wa.030
+sc.30 gq.21 il.00.V b.110.S b.111.S b.112.S b.113.S b.020.S b.021.S b.022.S b.023.S gi.30.V sc.31 gq.30
+il.10.V gi.31.V qc.00 qt.01 qt.10 xq.1 xt.20.S xt.21.S tr.020.S tr.021.S tr.110.S tr.111.S wa.001 wa.011
+wa.021 wa.031 gq.31 il.01.V qc.10 b.120.S b.121.S b.122.S b.123.S b.030.S b.031.S b.032.S b.033.S il.11.V
+xq.2 qc.01 qt.02 ui.0.V ui.1.V uq.0 qc.11 uq.1 qt.11 xt.30.S xt.31.S tr.030.S tr.031.S tr.120.S
+tr.121.S wa.002 wa.012 wa.022 wa.032 b.130.S b.131.S b.132.S b.133.S o.00.S o.01.S o.02.S o.03.S il.02.V
+xq.3 qt.03 il.12.V qc.02 qt.12 tr.130.S tr.131.S wa.003 wa.013 wa.023 wa.033 wv.00.S wv.01.S wv.02.S
+wv.03.S o.10.S o.11.S o.12.S o.13.S qt.13 qc.12 il.03.V il.13.V qc.03 qc.13 wa.100 wa.101 wa.102
+wa.103 wv.10.S wa.110 wa.111 wa.112 wa.113 wv.11.V wa.120 wa.121 wa.122 wa.123 wv.12.S wa.130 wa.131
+wa.132 wa.133 wv.13.V o.20.S o.21.S o.22.S o.23.S o.30.S o.31.V o.32.S o.33.V
 """
 
 
@@ -58,7 +56,7 @@ def tile_afnb_pb_v_kernel(
         psum = ctx.enter_context(tc.psum_pool(name="psum", bufs=8))
 
         def bank():
-            t = psum.tile([128, 512], F32, name="bank")
+            t = psum.tile([128, 512], F32, name="bank", bufs=4)
             return t
 
         def evac(eng, out, in_):
@@ -72,36 +70,31 @@ def tile_afnb_pb_v_kernel(
             scales = work.tile([128, 512], U8, name=name + "_scales", align_bytes=64, bufs=bufs)
             return codes, scales
 
-        def quant(dst, fmt, src, n0=0, n1=512):
+        def quant(dst, fmt, src):
             nc.vector.quantize_mx(
-                out=dst[0][:, n0:n1].bitcast(fmt),
-                scales=dst[1][:, n0:n1],
-                in_=src[:, n0:n1, :].rearrange("p n j -> p (n j)"),
+                out=dst[0][:].bitcast(fmt), scales=dst[1][:], in_=src[:].rearrange("p n j -> p (n j)")
             )
 
-        def inter():
-            t = work.tile([128, 512, 4], BF16, name="inter", align_bytes=64, bufs=NINTER)
+        def inter(name="mixed", bufs=4):
+            t = work.tile([128, 512, 4], BF16, name=name, align_bytes=64, bufs=bufs)
             return t
 
         D = {}
 
         def keyed(*key):
             if key not in D:
-                D[key] = inter()
+                D[key] = inter("chan", 3) if key[0] == "c" else inter()
             return D[key]
 
-        def interleave(eng, dst, src, f):
-            n = slice(256 * f, 256 * f + 256)
+        def interleave(eng, dst, src):
             evac(
                 eng,
-                dst[:, n, :].rearrange("p (c i) j -> p c j i", i=4),
-                src[:, :, n].rearrange("p j (c i) -> p c j i", i=4),
+                dst[:].rearrange("p (c i) j -> p c j i", i=4),
+                src[:].rearrange("p j (c i) -> p c j i", i=4),
             )
 
         ident = keep.tile([128, 128], F32, name="ident")
         make_identity(nc, ident[:])
-        ident_bf = keep.tile([128, 128], BF16, name="ident_bf")
-        make_identity(nc, ident_bf[:])
 
         gf_t = keep.tile([128, 2, 4], BF16, name="gf_t")
         rs_t = keep.tile([128, 2, 4], F32, name="rs_t")
@@ -123,19 +116,19 @@ def tile_afnb_pb_v_kernel(
             graw[T, q] = t[:]
 
         def load_gg(b, q):
-            t = work.tile([128, 4, 1024], BF16, name="rawL", bufs=4)
+            t = work.tile([128, 4, 1024], BF16, name="rawL", bufs=2)
             nc.sync.dma_start(out=t[:], in_=g_v[b, q])
             for i in range(2):
                 graw[2 * b + i, q] = t[:, :, 512 * i : 512 * i + 512]
 
-        def load_x(b):
-            t = work.tile([128, 4, 1024], BF16, name="rawL", bufs=4)
-            nc.sync.dma_start(out=t[:], in_=x_v[b])
-            for i in range(2):
-                xraw[2 * b + i] = t[:, :, 512 * i : 512 * i + 512]
+        def load_x(T):
+            t = work.tile([128, 4, 512], BF16, name="raw", bufs=NRAW)
+            n0 = 512 * (T % 2)
+            nc.sync.dma_start(out=t[:], in_=x_v[T // 2, :, :, n0 : n0 + 512])
+            xraw[T] = t[:]
 
         def load_u(q):
-            t = work.tile([128, 4, 512], BF16, name="rawu", bufs=2)
+            t = work.tile([128, 4, 512], BF16, name="raw", bufs=NRAW)
             nc.sync.dma_start(out=t[:], in_=ww_v[q])
             uraw[q] = t
 
@@ -159,31 +152,19 @@ def tile_afnb_pb_v_kernel(
         def cols(t):
             return slice(128 * t, 128 * t + 128)
 
-        def wi(h, q, f, eng):
-            bk = psum.tile([128, 2, 128, 4], BF16, name="bank")
-            src = wraw[h, q][:].rearrange("p j (m t) -> p t m j", t=4)
-            for i in range(2):
-                nc.tensor.matmul(
-                    out=bk[:, i].rearrange("p m j -> p (m j)"),
-                    lhsT=ident_bf[:],
-                    rhs=src[:, 2 * f + i],
-                    start=True,
-                    stop=True,
-                )
-            d = keyed("w", h, q)
+        def wi(h, q, eng):
             evac(
                 eng,
-                d[:, 256 * f : 256 * f + 256].rearrange("p n j -> p (n j)"),
-                bk[:].rearrange("p i m j -> p (i m j)"),
+                keyed("w", h, q)[:].rearrange("p (t m) j -> p t m j", t=4),
+                wraw[h, q][:].rearrange("p j (m t) -> p t m j", t=4),
             )
 
-        def w_quant(h, q, f):
-            if (h, q) not in wq:
-                wq[h, q] = coded("w", 4)
-            quant(wq[h, q], E4X4, D["w", h, q], 256 * f, 256 * f + 256)
+        def w_quant(h, q):
+            wq[h, q] = coded("w", 4)
+            quant(wq[h, q], E4X4, D["w", h, q])
 
-        def ui(q, f, eng):
-            interleave(eng, keyed("u", q, 0), uraw[q], f)
+        def ui(q, eng):
+            interleave(eng, keyed("u", q, 0), uraw[q])
 
         def u_quant(q):
             uq[q] = coded("u", 2)
@@ -201,8 +182,8 @@ def tile_afnb_pb_v_kernel(
                     op0=MULT,
                 )
 
-        def gi(T, q, f, eng):
-            interleave(eng, keyed("g", T, q), Z[T, q], f)
+        def gi(T, q, eng):
+            interleave(eng, keyed("g", T, q), Z[T, q])
 
         def g_quant(T, q):
             gq[T, q] = coded("g", 6)
@@ -210,7 +191,7 @@ def tile_afnb_pb_v_kernel(
 
         def xt(T, h, eng):
             if T not in XD:
-                XD[T] = inter()
+                XD[T] = inter("turned", NTURN)
             d = XD[T]
             bk = bank()
             for r in range(2):
@@ -241,7 +222,7 @@ def tile_afnb_pb_v_kernel(
         def tr(h, T, hh, eng):
             e = E[h, T]
             if (h, T) not in TD:
-                TD[h, T] = inter()
+                TD[h, T] = inter("turned", NTURN)
             bk = bank()
             for r in range(2):
                 for u in range(2):
@@ -252,17 +233,16 @@ def tile_afnb_pb_v_kernel(
                     )
             evac(eng, words(TD[h, T])[:, 2 * hh : 2 * hh + 2], bk[:].rearrange("p (r u v) -> p r v u", r=2, u=2))
 
-        def il(h, T, f, eng):
-            interleave(eng, keyed("c", h, T), E[h, T], f)
+        def il(h, T, eng):
+            interleave(eng, keyed("c", h, T), E[h, T])
 
         def qc(h, T):
             ckq[h, T] = coded("ck", 5)
             quant(ckq[h, T], E5X4, D["c", h, T])
 
-        def qt(h, T, f):
-            if (h, T) not in tkq:
-                tkq[h, T] = coded("tk", 8)
-            quant(tkq[h, T], E5X4, TD[h, T], 256 * f, 256 * f + 256)
+        def qt(h, T):
+            tkq[h, T] = coded("tk", 8)
+            quant(tkq[h, T], E5X4, TD[h, T])
 
         def o(T, r, eng):
             bk = bank()
@@ -281,7 +261,7 @@ def tile_afnb_pb_v_kernel(
 
         def wa(h, t, T):
             if T == 0:
-                wbank[h, t] = bank()
+                wbank[h, t] = psum.tile([128, 512], F32, name="acc", bufs=4)
             mm(wbank[h, t], tkq[h, T], cols(t), xq[T], T == 0, T == 3, E5X4, E4X4)
 
         def wv(h, t, eng):

@@ -15,27 +15,18 @@ FLOPS = 2 * 2048 * (1024 * 1024 + 2 * 1024 * 512)
 BYTES = 2 * (2048 * 1024 + 2048 * 512 + 1024 * 1024 + 1024 * 512) + 4 * (2048 * 512 + 1024 * 512)
 
 
-NTURN = 5
+NTURN = 6
 NRAW = 11
-NE = 5
-LOADS = """
-
-"""
+NE = 6
+LOADS = ""
 PLAN = """
-lw.00 lg.00 lw.01 lg.01 lg.10 lw.10 lg.11 lw.11 lx.0 lG.10 lG.11 lx.1 lu.0 st.
-wi.00.V sc.00 wq.00 gi.00.V wi.01.S sc.01 gq.00 gi.01.V wq.01 gq.01 wi.10.S wi.11.S sc.10 b.000.S
-b.001.S b.002.S b.003.S gi.10.V sc.11 gq.10 gi.11.V wq.10 wq.11 xt.00.S xt.01.S tr.000.S tr.001.S lu.1
-lx.2 lx.3 sc.20 gq.11 b.100.S b.101.S b.102.S b.103.S b.010.S b.011.S b.012.S b.013.S gi.20.V sc.21
-gq.20 xq.0 gi.21.V qt.00 xt.10.S xt.11.S tr.010.S tr.011.S tr.100.S tr.101.S wa.000 wa.010 wa.020 wa.030
-sc.30 gq.21 il.00.V b.110.S b.111.S b.112.S b.113.S b.020.S b.021.S b.022.S b.023.S gi.30.V sc.31 gq.30
-il.10.V gi.31.V qc.00 qt.01 qt.10 xq.1 xt.20.S xt.21.S tr.020.S tr.021.S tr.110.S tr.111.S wa.001 wa.011
-wa.021 wa.031 gq.31 il.01.V qc.10 b.120.S b.121.S b.122.S b.123.S b.030.S b.031.S b.032.S b.033.S il.11.V
-xq.2 qc.01 qt.02 ui.0.V ui.1.V uq.0 qc.11 uq.1 qt.11 xt.30.S xt.31.S tr.030.S tr.031.S tr.120.S
-tr.121.S wa.002 wa.012 wa.022 wa.032 b.130.S b.131.S b.132.S b.133.S o.00.S o.01.S o.02.S o.03.S il.02.V
-xq.3 qt.03 il.12.V qc.02 qt.12 tr.130.S tr.131.S wa.003 wa.013 wa.023 wa.033 wv.00.S wv.01.S wv.02.S
-wv.03.S o.10.S o.11.S o.12.S o.13.S qt.13 qc.12 il.03.V il.13.V qc.03 qc.13 wa.100 wa.101 wa.102
-wa.103 wv.10.S wa.110 wa.111 wa.112 wa.113 wv.11.V wa.120 wa.121 wa.122 wa.123 wv.12.S wa.130 wa.131
-wa.132 wa.133 wv.13.V o.20.S o.21.S o.22.S o.23.S o.30.S o.31.V o.32.S o.33.V
+lg.00 lw.00 lg.01 lw.01 lg.10 lg.11 lx.0 lw.10 lw.11 lG.10 lG.11 lx.2
+st. sc.00 gi.00.V gq.00 wi.00.S sc.01 wq.00 wi.01.V gi.01.S sc.10 wq.01 gq.01 sc.11 gi.10.S gi.11.V
+B.00.S gq.10 X.0.S wi.10.V gq.11 wi.11.V lx.3 wq.10 wq.11 R.00.S sc.20 il.00.V
+B.01.S B.10.S qt.00 sc.21 lx.1 xq.0 B.11.S lu.0 WA.0 qc.00 gi.20.V gi.21.V R.01.S X.1.S sc.30 gq.20 sc.31 gi.30.V gq.21 lu.1 X.2.S R.11.S xq.1 R.10.S qt.01 X.3.S gi.31.V gq.30 gq.31
+B.02.S il.10.V B.12.S B.13.S ui.1.V xq.2 ui.0.V uq.1 il.01.V il.11.V uq.0 WA.1 qc.11 qc.10
+B.03.S xq.3 R.02.SV R.03.S qt.11 R.12.V qt.03 R.13.S qt.02 qc.01 O.0.S il.12.V O.1.S il.02.V qt.12 qc.12 WA.2 qc.02 WA.3 qt.13 qt.10 WV..S
+O.2.S il.13.V il.03.V qc.13 qc.03 W.0.S W.1.V O.3.V W.2.S W.3.S
 """
 
 
@@ -277,7 +268,40 @@ def tile_afnb_pb_v_kernel(
                 op=MULT,
             )
 
+        def eb(e, k):
+            return e[k % len(e)]
+
+        def B(h, T, e):
+            for t in range(4):
+                b(h, T, t, eb(e, t))
+
+        def R(h, T, e):
+            for hh in range(2):
+                tr(h, T, hh, eb(e, hh))
+
+        def X(T, e):
+            for h in range(2):
+                xt(T, h, eb(e, h))
+
+        def O(T, e):
+            for r in range(4):
+                o(T, r, eb(e, r))
+
+        def WA(T):
+            for t in range(4):
+                wa(0, t, T)
+
+        def WV(e):
+            for t in range(4):
+                wv(0, t, eb(e, t))
+
+        def W(t, e):
+            for T in range(4):
+                wa(1, t, T)
+            wv(1, t, e)
+
         ops = {
+            "B": B, "R": R, "X": X, "O": O, "WA": WA, "WV": WV, "W": W,
             "lw": load_w, "lg": load_g, "lx": load_x, "lu": load_u, "lG": load_gg,
             "wi": wi, "wq": w_quant, "ui": ui, "uq": u_quant, "sc": sc, "gi": gi, "gq": g_quant,
             "xt": xt, "xq": x_quant, "b": b, "tr": tr, "il": il, "qc": qc, "qt": qt, "o": o, "wa": wa, "wv": wv, "st": st,

@@ -7,315 +7,386 @@ F32 = mybir.dt.float32
 BF16 = mybir.dt.bfloat16
 U32 = mybir.dt.uint32
 U8 = mybir.dt.uint8
-E4X4 = mybir.dt.float8_e4m3fn_x4
-E5X4 = mybir.dt.float8_e5m2_x4
-MULT = mybir.AluOpType.mult
+E4M3 = mybir.dt.float8_e4m3fn_x4
+E5M2 = mybir.dt.float8_e5m2_x4
 
-FLOPS = 2 * 2048 * (1024 * 1024 + 2 * 1024 * 512)
-BYTES = 2 * (2048 * 1024 + 2048 * 512 + 1024 * 1024 + 1024 * 512) + 4 * (2048 * 512 + 1024 * 512)
+P = 128
+TOKENS = 2048
+OUT_CH = 1024
+CTX_CH = 512
+BLOCK = 512
 
-
-NTURN = 6
-NRAW = 11
-NE = 6
-LOADS = ""
-PLAN = """
-lg.00 lw.00 lg.01 lw.01 lg.10 lg.11 lx.0 lw.10 lw.11 lG.10 lG.11 lx.2
-st. sc.00 gi.00.V gq.00 wi.00.S sc.01 wq.00 wi.01.V gi.01.S sc.10 wq.01 gq.01 sc.11 gi.10.S gi.11.V
-B.00.S gq.10 X.0.S wi.10.V gq.11 wi.11.V lx.3 wq.10 wq.11 R.00.S sc.20 il.00.V
-B.01.S B.10.S qt.00 sc.21 lx.1 xq.0 B.11.S lu.0 WA.0 qc.00 gi.20.V gi.21.V R.01.S X.1.S sc.30 gq.20 sc.31 gi.30.V gq.21 lu.1 X.2.S R.11.S xq.1 R.10.S qt.01 X.3.S gi.31.V gq.30 gq.31
-B.02.S il.10.V B.12.S B.13.S ui.1.V xq.2 ui.0.V uq.1 il.01.V il.11.V uq.0 WA.1 qc.11 qc.10
-B.03.S xq.3 R.02.SV R.03.S qt.11 R.12.V qt.03 R.13.S qt.02 qc.01 O.0.S il.12.V O.1.S il.02.V qt.12 qc.12 WA.2 qc.02 WA.3 qt.13 qt.10 WV..S
-O.2.S il.13.V il.03.V qc.13 qc.03 W.0.S W.1.V O.3.V W.2.S W.3.S
-"""
+FLOPS = 2 * TOKENS * (OUT_CH * OUT_CH + 2 * OUT_CH * CTX_CH)
+BYTES = 2 * (TOKENS * OUT_CH + TOKENS * CTX_CH + OUT_CH * OUT_CH + OUT_CH * CTX_CH) + 4 * (
+    TOKENS * CTX_CH + OUT_CH * CTX_CH
+)
 
 
 def tile_afnb_pb_v_kernel(
     tc, context, high_feats, ww, bw, wf, bfuse, gf, bef, mf, vf, rstd, grad_out, out_0, out_1
 ):
     nc = tc.nc
-    g_v = grad_out.rearrange("b (q p j) h w -> b q p j (h w)", q=2, j=4)
-    x_v = context.rearrange("b (r p) h w -> b p r (h w)", p=128)
-    wf_v = wf.rearrange("(q p j) c -> q p j c", q=2, j=4)
-    ww_v = ww.rearrange("(q p j) v -> q p j v", q=2, j=4)
-    out0_v = out_0.rearrange("b (r p) h w -> b r p (h w)", p=128)
-    out1_v = out_1.rearrange("(h m t) v -> h t m v", h=2, t=4)
+
+    g_view = grad_out.rearrange("b (q p j) y x -> b q p j (y x)", q=2, j=4)
+    x_view = context.rearrange("b (r p) y x -> b p r (y x)", p=P)
+    wf_view = wf.rearrange("(q p j) c -> q p j c", q=2, j=4)
+    ww_view = ww.rearrange("(h p j) v -> h p j v", h=2, j=4)
+    out0_view = out_0.rearrange("b (r p) y x -> b r p (y x)", p=P)
+    out1_view = out_1.rearrange("(h m t) v -> h t m v", h=2, t=4)
+
+    def image_columns(n):
+        return slice(BLOCK * (n % 2), BLOCK * (n % 2) + BLOCK)
+
+    S = (nc.scalar.copy,)
+    V = (nc.vector.tensor_copy,)
+    SV = (nc.scalar.copy, nc.vector.tensor_copy)
 
     with ExitStack() as ctx:
         keep = ctx.enter_context(tc.tile_pool(name="keep", bufs=1))
-        work = ctx.enter_context(tc.tile_pool(name="work", bufs=3))
-        psum = ctx.enter_context(tc.psum_pool(name="psum", bufs=8))
+        work = ctx.enter_context(tc.tile_pool(name="work", bufs=1))
+        psum = ctx.enter_context(tc.psum_pool(name="psum", bufs=4))
 
-        def bank():
-            t = psum.tile([128, 512], F32, name="bank", bufs=4)
-            return t
+        def rotating_bank():
+            bank = psum.tile([P, BLOCK], F32, name="bank")
+            return bank
 
-        def evac(eng, out, in_):
-            if eng == "S":
-                nc.scalar.copy(out=out, in_=in_)
-            else:
-                nc.vector.tensor_copy(out=out, in_=in_)
+        def out1_bank():
+            bank = psum.tile([P, BLOCK], F32, name="out1_bank")
+            return bank
 
-        def coded(name, bufs):
-            codes = work.tile([128, 512], U32, name=name + "_codes", align_bytes=64, bufs=bufs)
-            scales = work.tile([128, 512], U8, name=name + "_scales", align_bytes=64, bufs=bufs)
+        def loaded(source):
+            tile = work.tile([P, 4, BLOCK], BF16, name="loaded", bufs=11)
+            nc.sync.dma_start(out=tile[:], in_=source)
+            return tile[:]
+
+        def grouped(name, bufs):
+            tile = work.tile([P, BLOCK, 4], BF16, name=name, align_bytes=64, bufs=bufs)
+            return tile
+
+        def quantized(name, bufs, fmt, source):
+            codes = work.tile([P, BLOCK], U32, name=name + "_codes", align_bytes=64, bufs=bufs)
+            scales = work.tile([P, BLOCK], U8, name=name + "_scales", align_bytes=64, bufs=bufs)
+            nc.vector.quantize_mx(
+                out=codes[:].bitcast(fmt), scales=scales[:], in_=source[:].rearrange("p n j -> p (n j)")
+            )
             return codes, scales
 
-        def quant(dst, fmt, src):
-            nc.vector.quantize_mx(
-                out=dst[0][:].bitcast(fmt), scales=dst[1][:], in_=src[:].rearrange("p n j -> p (n j)")
+        def group_by_four(copies, target, source):
+            copies[0](
+                out=target[:].rearrange("p (c i) j -> p c j i", i=4),
+                in_=source.rearrange("p j (c i) -> p c j i", i=4),
             )
 
-        def inter(name="mixed", bufs=4):
-            t = work.tile([128, 512, 4], BF16, name=name, align_bytes=64, bufs=bufs)
-            return t
-
-        D = {}
-
-        def keyed(*key):
-            if key not in D:
-                D[key] = inter("chan", 3) if key[0] == "c" else inter()
-            return D[key]
-
-        def interleave(eng, dst, src):
-            evac(
-                eng,
-                dst[:].rearrange("p (c i) j -> p c j i", i=4),
-                src[:].rearrange("p j (c i) -> p c j i", i=4),
-            )
-
-        ident = keep.tile([128, 128], F32, name="ident")
-        make_identity(nc, ident[:])
-
-        gf_t = keep.tile([128, 2, 4], BF16, name="gf_t")
-        rs_t = keep.tile([128, 2, 4], F32, name="rs_t")
-        s_t = keep.tile([128, 8], F32, name="s_t")
-        nc.sync.dma_start(out=gf_t[:], in_=gf.rearrange("(q p j) -> p q j", q=2, j=4))
-        nc.sync.dma_start(out=rs_t[:], in_=rstd.rearrange("(q p j) -> p q j", q=2, j=4))
-
-        wraw, graw, xraw, uraw = {}, {}, {}, {}
-
-        def load_w(h, q):
-            t = work.tile([128, 4, 512], BF16, name="raw", bufs=NRAW)
-            nc.sync.dma_start(out=t[:], in_=wf_v[q, :, :, 512 * h : 512 * h + 512])
-            wraw[h, q] = t
-
-        def load_g(T, q):
-            t = work.tile([128, 4, 512], BF16, name="raw", bufs=NRAW)
-            n0 = 512 * (T % 2)
-            nc.sync.dma_start(out=t[:], in_=g_v[T // 2, q, :, :, n0 : n0 + 512])
-            graw[T, q] = t[:]
-
-        def load_gg(b, q):
-            t = work.tile([128, 4, 1024], BF16, name="rawL", bufs=2)
-            nc.sync.dma_start(out=t[:], in_=g_v[b, q])
-            for i in range(2):
-                graw[2 * b + i, q] = t[:, :, 512 * i : 512 * i + 512]
-
-        def load_x(T):
-            t = work.tile([128, 4, 512], BF16, name="raw", bufs=NRAW)
-            n0 = 512 * (T % 2)
-            nc.sync.dma_start(out=t[:], in_=x_v[T // 2, :, :, n0 : n0 + 512])
-            xraw[T] = t[:]
-
-        def load_u(q):
-            t = work.tile([128, 4, 512], BF16, name="raw", bufs=NRAW)
-            nc.sync.dma_start(out=t[:], in_=ww_v[q])
-            uraw[q] = t
-
-
-        wq, gq, xq, uq, ckq, tkq, E, Z, XD, TD = {}, {}, {}, {}, {}, {}, {}, {}, {}, {}
-
-        def words(d):
-            return d[:].rearrange("p n j -> p (n j)").bitcast(F32).rearrange("p (a b u) -> p a b u", a=4, u=2)
-
-        def mm(bk, a, ac, b, start, stop, fa, fb):
+        def multiply(out, stationary, fmt_s, m, moving, fmt_m, start, stop):
+            columns = slice(P * m, P * m + P)
             nc.tensor.matmul_mx(
-                out=bk[:],
-                lhsT=a[0][:, ac].bitcast(fa),
-                lhsT_scale=a[1][:, ac],
-                rhs=b[0][:].bitcast(fb),
-                rhs_scale=b[1][:],
+                out=out,
+                lhsT=stationary[0][:, columns].bitcast(fmt_s),
+                lhsT_scale=stationary[1][:, columns],
+                rhs=moving[0][:].bitcast(fmt_m),
+                rhs_scale=moving[1][:],
                 start=start,
                 stop=stop,
             )
 
-        def cols(t):
-            return slice(128 * t, 128 * t + 128)
-
-        def wi(h, q, eng):
-            evac(
-                eng,
-                keyed("w", h, q)[:].rearrange("p (t m) j -> p t m j", t=4),
-                wraw[h, q][:].rearrange("p j (m t) -> p t m j", t=4),
+        def turn(target, f, word_block, copies):
+            bank = rotating_bank()
+            for r in range(2):
+                for u in range(2):
+                    nc.tensor.transpose(
+                        bank[:, 256 * r + P * u : 256 * r + P * u + P], word_block(2 * f + r, u), ident[:]
+                    )
+            words = target[:].rearrange("p n k -> p (n k)").bitcast(F32)
+            words = words.rearrange("p (r row u) -> p r row u", r=4, u=2)
+            copies[f % len(copies)](
+                out=words[:, 2 * f : 2 * f + 2], in_=bank[:].rearrange("p (r u row) -> p r row u", r=2, u=2)
             )
 
-        def w_quant(h, q):
-            wq[h, q] = coded("w", 4)
-            quant(wq[h, q], E4X4, D["w", h, q])
+        gf_tile = keep.tile([P, 2, 4], BF16, name="gf_tile")
+        rstd_tile = keep.tile([P, 2, 4], F32, name="rstd_tile")
+        factor = keep.tile([P, 8], F32, name="factor")
+        nc.sync.dma_start(out=gf_tile[:], in_=gf.rearrange("(q p j) -> p q j", q=2, j=4))
+        nc.sync.dma_start(out=rstd_tile[:], in_=rstd.rearrange("(q p j) -> p q j", q=2, j=4))
+        ident = keep.tile([P, P], F32, name="ident")
+        make_identity(nc, ident[:])
 
-        def ui(q, eng):
-            interleave(eng, keyed("u", q, 0), uraw[q])
+        g_raw, g_image, g_mixed, g_mx = {}, {}, {}, {}
+        wc_raw, wc_mixed, wc_mx = {}, {}, {}
+        ww_raw, ww_mixed, ww_mx = {}, {}, {}
+        x_raw, x_sorted, x_turned, x_mx = {}, {}, {}, {}
+        dz1, dz1_turned, dz1_mixed, dz1_by_token, dz1_by_channel = {}, {}, {}, {}, {}
+        half0_bank = {}
 
-        def u_quant(q):
-            uq[q] = coded("u", 2)
-            quant(uq[q], E4X4, D["u", q, 0])
+        def load_g(n, q):
+            g_raw[n, q] = loaded(g_view[n // 2, q, :, :, image_columns(n)])
 
-        def sc(T, q):
-            z = work.tile([128, 4, 512], BF16, name="dz2", bufs=3)
-            Z[T, q] = z
+        def load_g_image1(q):
+            tile = work.tile([P, 4, 2 * BLOCK], BF16, name="g_image1", bufs=2)
+            nc.sync.dma_start(out=tile[:], in_=g_view[1, q])
+            g_image[q] = tile[:]
+            for n in (2, 3):
+                g_raw[n, q] = tile[:, :, image_columns(n)]
+
+        def load_wc(h, q):
+            wc_raw[h, q] = loaded(wf_view[q, :, :, BLOCK * h : BLOCK * h + BLOCK])
+
+        def load_ww(h):
+            ww_raw[h] = loaded(ww_view[h])
+
+        def load_x(n):
+            x_raw[n] = loaded(x_view[n // 2, :, :, image_columns(n)])
+
+        def channel_factors():
+            nc.vector.tensor_tensor(
+                out=factor[:],
+                in0=gf_tile[:].rearrange("p q j -> p (q j)"),
+                in1=rstd_tile[:].rearrange("p q j -> p (q j)"),
+                op=mybir.AluOpType.mult,
+            )
+
+        def scale_rows(rows, q):
             for j in range(4):
                 nc.vector.tensor_scalar(
-                    out=z[:, j, :],
-                    in0=graw[T, q][:, j, :],
-                    scalar1=s_t[:, 4 * q + j : 4 * q + j + 1],
+                    out=rows[:, j, :],
+                    in0=rows[:, j, :],
+                    scalar1=factor[:, 4 * q + j : 4 * q + j + 1],
                     scalar2=None,
-                    op0=MULT,
+                    op0=mybir.AluOpType.mult,
                 )
 
-        def gi(T, q, eng):
-            interleave(eng, keyed("g", T, q), Z[T, q])
+        def scale_g(n, q):
+            scale_rows(g_raw[n, q], q)
 
-        def g_quant(T, q):
-            gq[T, q] = coded("g", 6)
-            quant(gq[T, q], E5X4, D["g", T, q])
+        def scale_g_image1(q):
+            scale_rows(g_image[q], q)
 
-        def xt(T, h, eng):
-            if T not in XD:
-                XD[T] = inter("turned", NTURN)
-            d = XD[T]
-            bk = bank()
-            for r in range(2):
-                for u in range(2):
-                    nc.tensor.transpose(
-                        bk[:, 256 * r + 128 * u : 256 * r + 128 * u + 128],
-                        xraw[T][:, 2 * h + r, :].bitcast(F32)[:, u:256:2],
-                        ident[:],
-                    )
-            evac(eng, words(d)[:, 2 * h : 2 * h + 2], bk[:].rearrange("p (r u v) -> p r v u", r=2, u=2))
+        def mix_g(n, q, copies):
+            g_mixed[n, q] = grouped("mixed", 4)
+            group_by_four(copies, g_mixed[n, q], g_raw[n, q])
 
-        def x_quant(T):
-            xq[T] = coded("x", 4)
-            quant(xq[T], E4X4, XD[T])
+        def quantize_g(n, q):
+            g_mx[n, q] = quantized("g", 6, E5M2, g_mixed[n, q])
 
-        def b(h, T, t, eng):
-            if (h, T) not in E:
-                E[h, T] = work.tile([128, 4, 512], BF16, name="E", bufs=NE)
-            bk = bank()
-            for q in range(2):
-                mm(bk, wq[h, q], cols(t), gq[T, q], q == 0, q == 1, E4X4, E5X4)
-            evac(
-                eng,
-                E[h, T][:, t, :].rearrange("p (u q e) -> p u q e", u=2, e=2),
-                bk[:].rearrange("p (q u e) -> p u q e", u=2, e=2),
+        def mix_wc(h, q, copies):
+            wc_mixed[h, q] = grouped("mixed", 4)
+            copies[0](
+                out=wc_mixed[h, q][:].rearrange("p (t m) j -> p t m j", t=4),
+                in_=wc_raw[h, q].rearrange("p j (m t) -> p t m j", t=4),
             )
 
-        def tr(h, T, hh, eng):
-            e = E[h, T]
-            if (h, T) not in TD:
-                TD[h, T] = inter("turned", NTURN)
-            bk = bank()
-            for r in range(2):
-                for u in range(2):
-                    nc.tensor.transpose(
-                        bk[:, 256 * r + 128 * u : 256 * r + 128 * u + 128],
-                        e[:, 2 * hh + r, :].bitcast(F32)[:, 128 * u : 128 * u + 128],
-                        ident[:],
-                    )
-            evac(eng, words(TD[h, T])[:, 2 * hh : 2 * hh + 2], bk[:].rearrange("p (r u v) -> p r v u", r=2, u=2))
+        def quantize_wc(h, q):
+            wc_mx[h, q] = quantized("wc", 4, E4M3, wc_mixed[h, q])
 
-        def il(h, T, eng):
-            interleave(eng, keyed("c", h, T), E[h, T])
+        def mix_ww(h, copies):
+            ww_mixed[h] = grouped("mixed", 4)
+            group_by_four(copies, ww_mixed[h], ww_raw[h])
 
-        def qc(h, T):
-            ckq[h, T] = coded("ck", 5)
-            quant(ckq[h, T], E5X4, D["c", h, T])
+        def quantize_ww(h):
+            ww_mx[h] = quantized("ww", 2, E4M3, ww_mixed[h])
 
-        def qt(h, T):
-            tkq[h, T] = coded("tk", 8)
-            quant(tkq[h, T], E5X4, TD[h, T])
-
-        def o(T, r, eng):
-            bk = bank()
-            for h in range(2):
-                mm(bk, uq[h], cols(r), ckq[h, T], h == 0, h == 1, E4X4, E5X4)
-            res = work.tile([128, 512], F32, name="res", bufs=6)
-            evac(
-                eng,
-                res[:].rearrange("p (q u e) -> p q u e", u=2, e=2),
-                bk[:].rearrange("p (u q e) -> p q u e", u=2, e=2),
-            )
-            n0 = 512 * (T % 2)
-            nc.sync.dma_start(out=out0_v[T // 2, r, :, n0 : n0 + 512], in_=res[:])
-
-        wbank = {}
-
-        def wa(h, t, T):
-            if T == 0:
-                wbank[h, t] = psum.tile([128, 512], F32, name="acc", bufs=4)
-            mm(wbank[h, t], tkq[h, T], cols(t), xq[T], T == 0, T == 3, E5X4, E4X4)
-
-        def wv(h, t, eng):
-            res = work.tile([128, 512], F32, name="res", bufs=6)
-            evac(eng, res[:], wbank[h, t][:])
-            nc.sync.dma_start(out=out1_v[h, t], in_=res[:])
-
-        def st():
-            nc.vector.tensor_tensor(
-                out=s_t[:],
-                in0=gf_t[:].rearrange("p q j -> p (q j)"),
-                in1=rs_t[:].rearrange("p q j -> p (q j)"),
-                op=MULT,
+        def sort_x(n, copies):
+            x_sorted[n] = work.tile([P, 2, 4, P], F32, name="x_sorted", bufs=2)
+            words = x_raw[n].rearrange("p r t -> p (r t)").bitcast(F32)
+            copies[0](
+                out=x_sorted[n][:].rearrange("p u r (b i) -> p u (r b) i", i=8),
+                in_=words.rearrange("p (rb u i) -> p u rb i", u=2, i=8),
             )
 
-        def eb(e, k):
-            return e[k % len(e)]
+        def turn_x(n, copies):
+            x_turned[n] = grouped("turned", 6)
+            for f in range(2):
+                turn(x_turned[n], f, lambda r, u: x_sorted[n][:, u, r, :], copies)
 
-        def B(h, T, e):
+        def quantize_x(n):
+            x_mx[n] = quantized("x", 4, E4M3, x_turned[n])
+
+        def stage_one(h, n, copies):
+            dz1[h, n] = work.tile([P, 4, BLOCK], BF16, name="dz1", bufs=6)
             for t in range(4):
-                b(h, T, t, eb(e, t))
+                bank = rotating_bank()
+                for q in range(2):
+                    multiply(bank[:], wc_mx[h, q], E4M3, t, g_mx[n, q], E5M2, q == 0, q == 1)
+                copies[t % len(copies)](
+                    out=dz1[h, n][:, t, :].rearrange("p (u b w) -> p u b w", u=2, w=16),
+                    in_=bank[:].rearrange("p (b u w) -> p u b w", u=2, w=16),
+                )
 
-        def R(h, T, e):
-            for hh in range(2):
-                tr(h, T, hh, eb(e, hh))
+        def turn_dz1(h, n, copies):
+            dz1_turned[h, n] = grouped("turned", 6)
+            for f in range(2):
+                turn(
+                    dz1_turned[h, n],
+                    f,
+                    lambda t, u: dz1[h, n][:, t, :].bitcast(F32)[:, P * u : P * u + P],
+                    copies,
+                )
 
-        def X(T, e):
-            for h in range(2):
-                xt(T, h, eb(e, h))
+        def quantize_dz1_tokens(h, n):
+            dz1_by_token[h, n] = quantized("dz1_token", 8, E5M2, dz1_turned[h, n])
 
-        def O(T, e):
+        def mix_dz1(h, n, copies):
+            dz1_mixed[h, n] = grouped("dz1_mixed", 3)
+            group_by_four(copies, dz1_mixed[h, n], dz1[h, n][:])
+
+        def quantize_dz1_channels(h, n):
+            dz1_by_channel[h, n] = quantized("dz1_channel", 5, E5M2, dz1_mixed[h, n])
+
+        def dcontext(n, copies):
             for r in range(4):
-                o(T, r, eb(e, r))
+                bank = rotating_bank()
+                for h in range(2):
+                    multiply(bank[:], ww_mx[h], E4M3, r, dz1_by_channel[h, n], E5M2, h == 0, h == 1)
+                result = work.tile([P, BLOCK], F32, name="result", bufs=6)
+                copies[r % len(copies)](
+                    out=result[:].rearrange("p (b u w) -> p b u w", u=2, w=16),
+                    in_=bank[:].rearrange("p (u b w) -> p b u w", u=2, w=16),
+                )
+                nc.sync.dma_start(out=out0_view[n // 2, r, :, image_columns(n)], in_=result[:])
 
-        def WA(T):
+        def add_dww(bank, h, t, n):
+            multiply(bank[:], dz1_by_token[h, n], E5M2, t, x_mx[n], E4M3, n == 0, n == 3)
+
+        def store_dww(bank, h, t, copies):
+            result = work.tile([P, BLOCK], F32, name="result", bufs=6)
+            copies[0](out=result[:], in_=bank[:])
+            nc.sync.dma_start(out=out1_view[h, t], in_=result[:])
+
+        def dww_half0_add(n):
             for t in range(4):
-                wa(0, t, T)
+                if n == 0:
+                    half0_bank[t] = out1_bank()
+                add_dww(half0_bank[t], 0, t, n)
 
-        def WV(e):
+        def dww_half0_store(copies):
             for t in range(4):
-                wv(0, t, eb(e, t))
+                store_dww(half0_bank[t], 0, t, copies)
 
-        def W(t, e):
-            for T in range(4):
-                wa(1, t, T)
-            wv(1, t, e)
+        def dww_half1(t, copies):
+            bank = out1_bank()
+            for n in range(4):
+                add_dww(bank, 1, t, n)
+            store_dww(bank, 1, t, copies)
 
-        ops = {
-            "B": B, "R": R, "X": X, "O": O, "WA": WA, "WV": WV, "W": W,
-            "lw": load_w, "lg": load_g, "lx": load_x, "lu": load_u, "lG": load_gg,
-            "wi": wi, "wq": w_quant, "ui": ui, "uq": u_quant, "sc": sc, "gi": gi, "gq": g_quant,
-            "xt": xt, "xq": x_quant, "b": b, "tr": tr, "il": il, "qc": qc, "qt": qt, "o": o, "wa": wa, "wv": wv, "st": st,
-        }
-
-        def runs(token):
-            parts = token.split(".")
-            args = [int(c) for c in parts[1]]
-            if len(parts) > 2:
-                args.append(parts[2])
-            ops[parts[0]](*args)
-
-        for token in LOADS.split():
-            runs(token)
         with tc.manual_schedule():
-            for token in PLAN.split():
-                runs(token)
+            load_g(0, 0)
+            load_g(0, 1)
+            load_wc(0, 0)
+            load_wc(0, 1)
+            load_wc(1, 0)
+            load_wc(1, 1)
+            load_g(1, 0)
+            load_g(1, 1)
+            load_x(0)
+            load_g_image1(0)
+            load_g_image1(1)
+            load_x(1)
+            load_x(2)
+
+            channel_factors()
+            scale_g(0, 0)
+            scale_g(0, 1)
+            mix_g(0, 0, S)
+            mix_wc(0, 0, S)
+            mix_g(0, 1, V)
+            mix_wc(1, 0, S)
+            quantize_g(0, 0)
+            quantize_g(0, 1)
+            mix_wc(0, 1, V)
+            quantize_wc(0, 0)
+            quantize_wc(0, 1)
+            mix_wc(1, 1, V)
+            quantize_wc(1, 0)
+            quantize_wc(1, 1)
+            scale_g(1, 0)
+
+            stage_one(0, 0, S)
+            scale_g(1, 1)
+            mix_g(1, 0, V)
+            stage_one(1, 0, S)
+            mix_g(1, 1, V)
+            turn_dz1(0, 0, S)
+            sort_x(0, V)
+            quantize_g(1, 0)
+            quantize_g(1, 1)
+            turn_dz1(1, 0, S)
+            turn_x(0, SV)
+
+            stage_one(0, 1, S)
+            scale_g_image1(0)
+            scale_g_image1(1)
+            sort_x(1, V)
+            stage_one(1, 1, S)
+            mix_g(2, 0, V)
+            mix_g(2, 1, V)
+            turn_x(1, SV)
+            load_ww(0)
+            quantize_g(2, 0)
+            quantize_g(2, 1)
+            turn_dz1(0, 1, S)
+            load_x(3)
+            turn_dz1(1, 1, S)
+            quantize_x(0)
+            quantize_x(1)
+            sort_x(2, V)
+            quantize_dz1_tokens(0, 0)
+            sort_x(3, V)
+            mix_dz1(0, 0, V)
+            mix_g(3, 0, V)
+            quantize_dz1_tokens(1, 0)
+
+            stage_one(0, 2, S)
+            stage_one(1, 2, S)
+            turn_x(2, V)
+            quantize_g(3, 0)
+            turn_dz1(0, 2, S)
+            quantize_dz1_tokens(0, 1)
+            mix_g(3, 1, V)
+            turn_dz1(1, 2, SV)
+            quantize_g(3, 1)
+            load_ww(1)
+            turn_x(3, S)
+            dww_half0_add(0)
+            dww_half0_add(1)
+            mix_ww(0, V)
+            quantize_dz1_channels(0, 0)
+            quantize_dz1_tokens(1, 1)
+            mix_dz1(1, 0, S)
+            mix_ww(1, V)
+            quantize_dz1_channels(1, 0)
+
+            stage_one(0, 3, S)
+            quantize_ww(0)
+            quantize_dz1_tokens(0, 2)
+            quantize_x(2)
+            quantize_ww(1)
+            stage_one(1, 3, S)
+            quantize_x(3)
+            mix_dz1(0, 1, V)
+            turn_dz1(0, 3, S)
+            mix_dz1(1, 1, V)
+            turn_dz1(1, 3, S)
+            quantize_dz1_tokens(0, 3)
+            quantize_dz1_channels(0, 1)
+            quantize_dz1_channels(1, 1)
+            dcontext(0, S)
+            quantize_dz1_tokens(1, 3)
+            dww_half0_add(2)
+            quantize_dz1_tokens(1, 2)
+            dww_half0_add(3)
+            dww_half0_store(S)
+
+            dww_half1(0, S)
+            mix_dz1(0, 2, V)
+            quantize_dz1_channels(0, 2)
+            mix_dz1(1, 2, V)
+            dcontext(1, S)
+            quantize_dz1_channels(1, 2)
+            dww_half1(1, S)
+            mix_dz1(0, 3, V)
+            dcontext(2, S)
+            mix_dz1(1, 3, V)
+            quantize_dz1_channels(0, 3)
+            quantize_dz1_channels(1, 3)
+            dww_half1(2, S)
+            dcontext(3, SV)
+            dww_half1(3, S)

from contextlib import ExitStack

import concourse.mybir as mybir
from concourse.masks import make_identity

F32 = mybir.dt.float32
BF16 = mybir.dt.bfloat16
U32 = mybir.dt.uint32
U8 = mybir.dt.uint8
E4M3 = mybir.dt.float8_e4m3fn_x4
E5M2 = mybir.dt.float8_e5m2_x4

P = 128
TOKENS = 2048
OUT_CH = 1024
CTX_CH = 512
BLOCK = 512

FLOPS = 2 * TOKENS * (OUT_CH * OUT_CH + 2 * OUT_CH * CTX_CH)
BYTES = 2 * (TOKENS * OUT_CH + TOKENS * CTX_CH + OUT_CH * OUT_CH + OUT_CH * CTX_CH) + 4 * (
    TOKENS * CTX_CH + OUT_CH * CTX_CH
)


def tile_afnb_pb_v_kernel(
    tc, context, high_feats, ww, bw, wf, bfuse, gf, bef, mf, vf, rstd, grad_out, out_0, out_1
):
    nc = tc.nc

    g_view = grad_out.rearrange("b (q p j) y x -> b q p j (y x)", q=2, j=4)
    x_view = context.rearrange("b (r p) y x -> b p r (y x)", p=P)
    wf_view = wf.rearrange("(q p j) c -> q p j c", q=2, j=4)
    ww_view = ww.rearrange("(h p j) v -> h p j v", h=2, j=4)
    out0_view = out_0.rearrange("b (r p) y x -> b r p (y x)", p=P)
    out1_view = out_1.rearrange("(h m t) v -> h t m v", h=2, t=4)

    def image_columns(n):
        return slice(BLOCK * (n % 2), BLOCK * (n % 2) + BLOCK)

    S = (nc.scalar.copy,)
    V = (nc.vector.tensor_copy,)
    SV = (nc.scalar.copy, nc.vector.tensor_copy)

    with ExitStack() as ctx:
        keep = ctx.enter_context(tc.tile_pool(name="keep", bufs=1))
        work = ctx.enter_context(tc.tile_pool(name="work", bufs=1))
        psum = ctx.enter_context(tc.psum_pool(name="psum", bufs=4))

        def rotating_bank():
            bank = psum.tile([P, BLOCK], F32, name="bank")
            return bank

        def out1_bank():
            bank = psum.tile([P, BLOCK], F32, name="out1_bank")
            return bank

        def loaded(source):
            tile = work.tile([P, 4, BLOCK], BF16, name="loaded", bufs=11)
            nc.sync.dma_start(out=tile[:], in_=source)
            return tile[:]

        def grouped(name, bufs):
            tile = work.tile([P, BLOCK, 4], BF16, name=name, align_bytes=64, bufs=bufs)
            return tile

        def quantized(name, bufs, fmt, source):
            codes = work.tile([P, BLOCK], U32, name=name + "_codes", align_bytes=64, bufs=bufs)
            scales = work.tile([P, BLOCK], U8, name=name + "_scales", align_bytes=64, bufs=bufs)
            nc.vector.quantize_mx(
                out=codes[:].bitcast(fmt), scales=scales[:], in_=source[:].rearrange("p n j -> p (n j)")
            )
            return codes, scales

        def group_by_four(copies, target, source):
            copies[0](
                out=target[:].rearrange("p (c i) j -> p c j i", i=4),
                in_=source.rearrange("p j (c i) -> p c j i", i=4),
            )

        def multiply(out, stationary, fmt_s, m, moving, fmt_m, start, stop):
            columns = slice(P * m, P * m + P)
            nc.tensor.matmul_mx(
                out=out,
                lhsT=stationary[0][:, columns].bitcast(fmt_s),
                lhsT_scale=stationary[1][:, columns],
                rhs=moving[0][:].bitcast(fmt_m),
                rhs_scale=moving[1][:],
                start=start,
                stop=stop,
            )

        def turn(target, f, word_block, copies):
            bank = rotating_bank()
            for r in range(2):
                for u in range(2):
                    nc.tensor.transpose(
                        bank[:, 256 * r + P * u : 256 * r + P * u + P], word_block(2 * f + r, u), ident[:]
                    )
            words = target[:].rearrange("p n k -> p (n k)").bitcast(F32)
            words = words.rearrange("p (r row u) -> p r row u", r=4, u=2)
            copies[f % len(copies)](
                out=words[:, 2 * f : 2 * f + 2], in_=bank[:].rearrange("p (r u row) -> p r row u", r=2, u=2)
            )

        gf_tile = keep.tile([P, 2, 4], BF16, name="gf_tile")
        rstd_tile = keep.tile([P, 2, 4], F32, name="rstd_tile")
        factor = keep.tile([P, 8], F32, name="factor")
        nc.sync.dma_start(out=gf_tile[:], in_=gf.rearrange("(q p j) -> p q j", q=2, j=4))
        nc.sync.dma_start(out=rstd_tile[:], in_=rstd.rearrange("(q p j) -> p q j", q=2, j=4))
        ident = keep.tile([P, P], F32, name="ident")
        make_identity(nc, ident[:])

        g_raw, g_image, g_mixed, g_mx = {}, {}, {}, {}
        wc_raw, wc_mixed, wc_mx = {}, {}, {}
        ww_raw, ww_mixed, ww_mx = {}, {}, {}
        x_raw, x_sorted, x_turned, x_mx = {}, {}, {}, {}
        dz1, dz1_turned, dz1_mixed, dz1_by_token, dz1_by_channel = {}, {}, {}, {}, {}
        half0_bank = {}

        def load_g(n, q):
            g_raw[n, q] = loaded(g_view[n // 2, q, :, :, image_columns(n)])

        def load_g_image1(q):
            tile = work.tile([P, 4, 2 * BLOCK], BF16, name="g_image1", bufs=2)
            nc.sync.dma_start(out=tile[:], in_=g_view[1, q])
            g_image[q] = tile[:]
            for n in (2, 3):
                g_raw[n, q] = tile[:, :, image_columns(n)]

        def load_wc(h, q):
            wc_raw[h, q] = loaded(wf_view[q, :, :, BLOCK * h : BLOCK * h + BLOCK])

        def load_ww(h):
            ww_raw[h] = loaded(ww_view[h])

        def load_x(n):
            x_raw[n] = loaded(x_view[n // 2, :, :, image_columns(n)])

        def channel_factors():
            nc.vector.tensor_tensor(
                out=factor[:],
                in0=gf_tile[:].rearrange("p q j -> p (q j)"),
                in1=rstd_tile[:].rearrange("p q j -> p (q j)"),
                op=mybir.AluOpType.mult,
            )

        def scale_rows(rows, q):
            for j in range(4):
                nc.vector.tensor_scalar(
                    out=rows[:, j, :],
                    in0=rows[:, j, :],
                    scalar1=factor[:, 4 * q + j : 4 * q + j + 1],
                    scalar2=None,
                    op0=mybir.AluOpType.mult,
                )

        def scale_g(n, q):
            scale_rows(g_raw[n, q], q)

        def scale_g_image1(q):
            scale_rows(g_image[q], q)

        def mix_g(n, q, copies):
            g_mixed[n, q] = grouped("mixed", 4)
            group_by_four(copies, g_mixed[n, q], g_raw[n, q])

        def quantize_g(n, q):
            g_mx[n, q] = quantized("g", 6, E5M2, g_mixed[n, q])

        def mix_wc(h, q, copies):
            wc_mixed[h, q] = grouped("mixed", 4)
            copies[0](
                out=wc_mixed[h, q][:].rearrange("p (t m) j -> p t m j", t=4),
                in_=wc_raw[h, q].rearrange("p j (m t) -> p t m j", t=4),
            )

        def quantize_wc(h, q):
            wc_mx[h, q] = quantized("wc", 4, E4M3, wc_mixed[h, q])

        def mix_ww(h, copies):
            ww_mixed[h] = grouped("mixed", 4)
            group_by_four(copies, ww_mixed[h], ww_raw[h])

        def quantize_ww(h):
            ww_mx[h] = quantized("ww", 2, E4M3, ww_mixed[h])

        def sort_x(n, copies):
            x_sorted[n] = work.tile([P, 2, 4, P], F32, name="x_sorted", bufs=2)
            words = x_raw[n].rearrange("p r t -> p (r t)").bitcast(F32)
            copies[0](
                out=x_sorted[n][:].rearrange("p u r (b i) -> p u (r b) i", i=8),
                in_=words.rearrange("p (rb u i) -> p u rb i", u=2, i=8),
            )

        def turn_x(n, copies):
            x_turned[n] = grouped("turned", 6)
            for f in range(2):
                turn(x_turned[n], f, lambda r, u: x_sorted[n][:, u, r, :], copies)

        def quantize_x(n):
            x_mx[n] = quantized("x", 4, E4M3, x_turned[n])

        def stage_one(h, n, copies):
            dz1[h, n] = work.tile([P, 4, BLOCK], BF16, name="dz1", bufs=6)
            for t in range(4):
                bank = rotating_bank()
                for q in range(2):
                    multiply(bank[:], wc_mx[h, q], E4M3, t, g_mx[n, q], E5M2, q == 0, q == 1)
                copies[t % len(copies)](
                    out=dz1[h, n][:, t, :].rearrange("p (u b w) -> p u b w", u=2, w=16),
                    in_=bank[:].rearrange("p (b u w) -> p u b w", u=2, w=16),
                )

        def turn_dz1(h, n, copies):
            dz1_turned[h, n] = grouped("turned", 6)
            for f in range(2):
                turn(
                    dz1_turned[h, n],
                    f,
                    lambda t, u: dz1[h, n][:, t, :].bitcast(F32)[:, P * u : P * u + P],
                    copies,
                )

        def quantize_dz1_tokens(h, n):
            dz1_by_token[h, n] = quantized("dz1_token", 8, E5M2, dz1_turned[h, n])

        def mix_dz1(h, n, copies):
            dz1_mixed[h, n] = grouped("dz1_mixed", 3)
            group_by_four(copies, dz1_mixed[h, n], dz1[h, n][:])

        def quantize_dz1_channels(h, n):
            dz1_by_channel[h, n] = quantized("dz1_channel", 5, E5M2, dz1_mixed[h, n])

        def dcontext(n, copies):
            for r in range(4):
                bank = rotating_bank()
                for h in range(2):
                    multiply(bank[:], ww_mx[h], E4M3, r, dz1_by_channel[h, n], E5M2, h == 0, h == 1)
                result = work.tile([P, BLOCK], F32, name="result", bufs=6)
                copies[r % len(copies)](
                    out=result[:].rearrange("p (b u w) -> p b u w", u=2, w=16),
                    in_=bank[:].rearrange("p (u b w) -> p b u w", u=2, w=16),
                )
                nc.sync.dma_start(out=out0_view[n // 2, r, :, image_columns(n)], in_=result[:])

        def add_dww(bank, h, t, n):
            multiply(bank[:], dz1_by_token[h, n], E5M2, t, x_mx[n], E4M3, n == 0, n == 3)

        def store_dww(bank, h, t, copies):
            result = work.tile([P, BLOCK], F32, name="result", bufs=6)
            copies[0](out=result[:], in_=bank[:])
            nc.sync.dma_start(out=out1_view[h, t], in_=result[:])

        def dww_half0_add(n):
            for t in range(4):
                if n == 0:
                    half0_bank[t] = out1_bank()
                add_dww(half0_bank[t], 0, t, n)

        def dww_half0_store(copies):
            for t in range(4):
                store_dww(half0_bank[t], 0, t, copies)

        def dww_half1(t, copies):
            bank = out1_bank()
            for n in range(4):
                add_dww(bank, 1, t, n)
            store_dww(bank, 1, t, copies)

        with tc.manual_schedule():
            load_g(0, 0)
            load_g(0, 1)
            load_wc(0, 0)
            load_wc(0, 1)
            load_wc(1, 0)
            load_wc(1, 1)
            load_g(1, 0)
            load_g(1, 1)
            load_x(0)
            load_g_image1(0)
            load_g_image1(1)
            load_x(1)
            load_x(2)

            channel_factors()
            scale_g(0, 0)
            scale_g(0, 1)
            mix_g(0, 0, S)
            mix_wc(0, 0, S)
            mix_g(0, 1, V)
            mix_wc(1, 0, S)
            quantize_g(0, 0)
            quantize_g(0, 1)
            mix_wc(0, 1, V)
            quantize_wc(0, 0)
            quantize_wc(0, 1)
            mix_wc(1, 1, V)
            quantize_wc(1, 0)
            quantize_wc(1, 1)
            scale_g(1, 0)

            stage_one(0, 0, S)
            scale_g(1, 1)
            mix_g(1, 0, V)
            stage_one(1, 0, S)
            mix_g(1, 1, V)
            turn_dz1(0, 0, S)
            sort_x(0, V)
            quantize_g(1, 0)
            quantize_g(1, 1)
            turn_dz1(1, 0, S)
            turn_x(0, SV)

            stage_one(0, 1, S)
            scale_g_image1(0)
            scale_g_image1(1)
            sort_x(1, V)
            stage_one(1, 1, S)
            mix_g(2, 0, V)
            mix_g(2, 1, V)
            turn_x(1, SV)
            load_ww(0)
            quantize_g(2, 0)
            quantize_g(2, 1)
            turn_dz1(0, 1, S)
            load_x(3)
            turn_dz1(1, 1, S)
            quantize_x(0)
            quantize_x(1)
            sort_x(2, V)
            quantize_dz1_tokens(0, 0)
            sort_x(3, V)
            mix_dz1(0, 0, V)
            mix_g(3, 0, V)
            quantize_dz1_tokens(1, 0)

            stage_one(0, 2, S)
            stage_one(1, 2, S)
            turn_x(2, V)
            quantize_g(3, 0)
            turn_dz1(0, 2, S)
            quantize_dz1_tokens(0, 1)
            mix_g(3, 1, V)
            turn_dz1(1, 2, SV)
            quantize_g(3, 1)
            load_ww(1)
            turn_x(3, S)
            dww_half0_add(0)
            dww_half0_add(1)
            mix_ww(0, V)
            quantize_dz1_channels(0, 0)
            quantize_dz1_tokens(1, 1)
            mix_dz1(1, 0, S)
            mix_ww(1, V)
            quantize_dz1_channels(1, 0)

            stage_one(0, 3, S)
            quantize_ww(0)
            quantize_dz1_tokens(0, 2)
            quantize_x(2)
            quantize_ww(1)
            stage_one(1, 3, S)
            quantize_x(3)
            mix_dz1(0, 1, V)
            turn_dz1(0, 3, S)
            mix_dz1(1, 1, V)
            turn_dz1(1, 3, S)
            quantize_dz1_tokens(0, 3)
            quantize_dz1_channels(0, 1)
            quantize_dz1_channels(1, 1)
            dcontext(0, S)
            quantize_dz1_tokens(1, 3)
            dww_half0_add(2)
            quantize_dz1_tokens(1, 2)
            dww_half0_add(3)
            dww_half0_store(S)

            dww_half1(0, S)
            mix_dz1(0, 2, V)
            quantize_dz1_channels(0, 2)
            mix_dz1(1, 2, V)
            dcontext(1, S)
            quantize_dz1_channels(1, 2)
            dww_half1(1, S)
            mix_dz1(0, 3, V)
            dcontext(2, S)
            mix_dz1(1, 3, V)
            quantize_dz1_channels(0, 3)
            quantize_dz1_channels(1, 3)
            dww_half1(2, S)
            dcontext(3, SV)
            dww_half1(3, S)
